import numpy as np
import ml_dtypes


def mxq(x, axis, fmt="e4m3"):
    dtype, down = {"e4m3": (ml_dtypes.float8_e4m3fn, 7), "e5m2": (ml_dtypes.float8_e5m2, 14)}[fmt]
    v = np.moveaxis(np.asarray(x, np.float32).astype(ml_dtypes.bfloat16).astype(np.float64), axis, -1)
    blocks = v.reshape(v.shape[:-1] + (-1, 32))
    amax = np.abs(blocks).max(-1, keepdims=True)
    byte = np.maximum(np.where(amax > 0, np.frexp(amax)[1] - 1 + 127, 0) - down, 1)
    scale = np.exp2(byte - 127.0)
    codes = (blocks / scale).astype(np.float32).astype(dtype).astype(np.float64)
    return np.moveaxis((codes * scale).reshape(v.shape), -1, axis)


WIDE = False


def mx_kscale(k):
    if not WIDE:
        return np.ones(k)
    levels = np.array([20, -20, 10, -10, 0])
    a = np.random.permutation(np.resize(levels, k // 512 * 4)).reshape(k // 512, 4)
    idx = np.arange(k)
    return np.exp2(a[idx // 512, idx % 128 // 32])


BF16 = ml_dtypes.bfloat16


def bf(x):
    return np.asarray(x, np.float32).astype(BF16)


def f64(x):
    return np.asarray(x).astype(np.float64)


N, C, O, OH, OW, KH, KW, STRIDE, PAD = 512, 128, 512, 3, 3, 3, 3, 1, 1
H, W = (OH - 1) * STRIDE + KH - 2 * PAD, (OW - 1) * STRIDE + KW - 2 * PAD
NEG_SLOPE = 0.1


def span(t, n_out, n_in):
    ok = [p for p in range(n_out) if 0 <= p * STRIDE + t - PAD < n_in]
    return ok[0], ok[-1] + 1


def preact(x, weight, bias):
    xf = f64(x)
    wt = f64(weight)[0]
    acc = np.zeros((N, O, OH, OW))
    for i in range(KH):
        h0, h1 = span(i, OH, H)
        a0 = h0 * STRIDE + i - PAD
        for j in range(KW):
            w0, w1 = span(j, OW, W)
            b0 = w0 * STRIDE + j - PAD
            xs = xf[:, :, a0:a0 + (h1 - h0 - 1) * STRIDE + 1:STRIDE, b0:b0 + (w1 - w0 - 1) * STRIDE + 1:STRIDE]
            ws = wt[:, :, h0:h1, w0:w1, i * KW + j]
            acc[:, :, h0:h1, w0:w1] += (xs.transpose(2, 3, 0, 1) @ ws.transpose(2, 3, 1, 0)).transpose(2, 3, 0, 1)
    return acc + f64(bias)


def setup_inputs():
    u = mx_kscale(O)
    x = bf(np.random.standard_normal((N, C, H, W)))
    w0 = bf(np.random.standard_normal((1, O, C, OH, OW, KH * KW)) * np.sqrt(2.0 / (KH * KW * C)))
    bias = bf(np.random.standard_normal((1, O, OH, OW)) * 0.3)
    g = bf(np.random.standard_normal((N, O, OH, OW)) * np.exp2(np.random.randint(-12, 1, (N, 1, OH, OW))) * 8.0 * u[None, :, None, None])
    z = preact(x, w0, bias)
    return {"x": x,
            "weight": bf(f64(w0) / u[None, :, None, None, None, None]),
            "bias": bias,
            "z": np.asarray(z, np.float32),
            "grad_out": g}


def reference(x, weight, bias, z, grad_out):
    dz = f64(grad_out) * np.where(f64(z) >= 0, 1.0, NEG_SLOPE)
    dq = mxq(dz, 1, "e5m2")
    wt = f64(weight)[0]
    gx = np.zeros((N, C, H, W))
    for i in range(KH):
        h0, h1 = span(i, OH, H)
        a0 = h0 * STRIDE + i - PAD
        for j in range(KW):
            w0, w1 = span(j, OW, W)
            b0 = w0 * STRIDE + j - PAD
            ds = dq[:, :, h0:h1, w0:w1]
            wq = mxq(wt[:, :, h0:h1, w0:w1, i * KW + j], 0, "e4m3")
            p = ds.transpose(2, 3, 0, 1) @ wq.transpose(2, 3, 0, 1)
            gx[:, :, a0:a0 + (h1 - h0 - 1) * STRIDE + 1:STRIDE, b0:b0 + (w1 - w0 - 1) * STRIDE + 1:STRIDE] += p.transpose(2, 3, 0, 1)
    return gx

@@ -1,0 +1,160 @@
+from contextlib import ExitStack
+
+import concourse.mybir as mybir
+from concourse.masks import make_identity
+
+F32 = mybir.dt.float32
+BF16 = mybir.dt.bfloat16
+U32 = mybir.dt.uint32
+U8 = mybir.dt.uint8
+I32 = mybir.dt.int32
+E4M3X4 = mybir.dt.float8_e4m3fn_x4
+E5M2X4 = mybir.dt.float8_e5m2_x4
+ALU = mybir.AluOpType
+
+P = 128
+PACK = 4
+N, C, O = 512, 128, 512
+SIDE = 3
+PLACES = SIDE * SIDE
+TAPS = SIDE * SIDE
+NEG_SLOPE = 0.1
+
+SLOTS = 4
+C_PART = 64
+PARTS = C // C_PART
+C_LOAD = 32
+N_COLS = PARTS * SLOTS * C_PART
+
+USED_TAPS = 49
+FLOPS = 2 * USED_TAPS * N * O * C
+BYTES = USED_TAPS * O * C * 2 + N * O * PLACES * (4 + 2) + N * C * PLACES * 4
+
+
+def near(v):
+    return range(max(0, v - 1), min(SIDE, v + 2))
+
+
+def tile_locallyconnected2d_t_v_kernel(tc, x, weight, bias, z, grad_out, out):
+    nc = tc.nc
+
+    w_rows = weight.rearrange("u (j p) c h w t -> p (u j) c (h w t)", p=P)
+    z_rows = z.rearrange("n (j p) h w -> (n j) (p h w)", j=PACK)
+    g_rows = grad_out.rearrange("n (j p) h w -> (n j) (p h w)", j=PACK)
+    out_rows = out.rearrange("n c a b -> n (c a b)")
+
+    passes = [(h, w, a) for a in range(SIDE) for h in near(a) for w in range(SIDE)]
+
+    with ExitStack() as ctx:
+        keep = ctx.enter_context(tc.tile_pool(name="keep", bufs=1))
+        w_raw_pool = ctx.enter_context(tc.tile_pool(name="w_raw", bufs=3))
+        w_stage_pool = ctx.enter_context(tc.tile_pool(name="w_stage", bufs=1))
+        load_pool = ctx.enter_context(tc.tile_pool(name="load", bufs=5))
+        work_pool = ctx.enter_context(tc.tile_pool(name="work", bufs=2))
+        dz_pool = ctx.enter_context(tc.tile_pool(name="dz", bufs=3))
+        turn_pool = ctx.enter_context(tc.psum_pool(name="turn", bufs=3))
+        acc_pool = ctx.enter_context(tc.psum_pool(name="acc", bufs=5))
+
+        ident = keep.tile([P, P], BF16)
+        make_identity(nc, ident[:])
+
+        w_codes = keep.tile([P, len(passes), PARTS, SLOTS, C_PART], U32, align_bytes=64)
+        w_scales = keep.tile([P, len(passes), PARTS, SLOTS, C_PART], U8, align_bytes=64)
+        nc.vector.memset(w_codes[:].bitcast(I32), 0)
+        nc.vector.memset(w_scales[:].bitcast(I32), 0)
+
+        for part in range(PARTS):
+            stage = w_stage_pool.tile([P, USED_TAPS, C_PART, PACK], BF16, align_bytes=64)
+            for c_lo in range(0, C_PART, C_LOAD):
+                raw = w_raw_pool.tile([P, PACK, C_LOAD, PLACES * TAPS], BF16)
+                c0 = part * C_PART + c_lo
+                nc.sync.dma_start(out=raw[:], in_=w_rows[:, :, c0 : c0 + C_LOAD, :])
+                slot = 0
+                for h, w, a in passes:
+                    cols = near(w)
+                    first = (SIDE * h + w) * TAPS + SIDE * (a - h + 1) + (cols[0] - w + 1)
+                    src = raw[:, :, :, first : first + len(cols)]
+                    dst = stage[:, slot : slot + len(cols), c_lo : c_lo + C_LOAD, :]
+                    if w == 1:
+                        nc.vector.tensor_copy(
+                            out=dst.rearrange("p b c j -> p c b j"),
+                            in_=src.rearrange("p j c b -> p c b j"),
+                        )
+                    else:
+                        nc.scalar.copy(
+                            out=dst.rearrange("p b c j -> p c b j"),
+                            in_=src.rearrange("p j c b -> p c b j"),
+                        )
+                    slot += len(cols)
+            slot = 0
+            for k, (h, w, a) in enumerate(passes):
+                cols = near(w)
+                for s in range(0, len(cols), 2):
+                    n_slots = min(2, len(cols) - s)
+                    b = cols[0] + s
+                    nc.vector.quantize_mx(
+                        out=w_codes[:, k, part, b : b + n_slots, :]
+                        .rearrange("p b c -> p (b c)")
+                        .bitcast(E4M3X4),
+                        scales=w_scales[:, k, part, b : b + n_slots, :].rearrange("p b c -> p (b c)"),
+                        in_=stage[:, slot + s : slot + s + n_slots, :, :].rearrange(
+                            "p b c j -> p (b c j)"
+                        ),
+                    )
+                slot += len(cols)
+
+        for block in range(N // P):
+            grouped = work_pool.tile([P, PLACES, PACK, P], BF16, align_bytes=64)
+            for r in range(PACK):
+                row0 = (block * PACK + r) * P
+                z_t = load_pool.tile([P, P * PLACES], F32)
+                nc.sync.dma_start(out=z_t[:], in_=z_rows[row0 : row0 + P, :])
+                g_t = load_pool.tile([P, P * PLACES], BF16)
+                nc.sync.dma_start(out=g_t[:], in_=g_rows[row0 : row0 + P, :])
+
+                slope = work_pool.tile([P, P * PLACES], F32)
+                nc.vector.tensor_scalar(
+                    out=slope[:], in0=z_t[:], scalar1=0.0, scalar2=NEG_SLOPE, op0=ALU.is_ge, op1=ALU.max
+                )
+                dz = dz_pool.tile([P, PLACES, P], BF16)
+                nc.vector.tensor_tensor(
+                    out=dz[:],
+                    in0=g_t[:].rearrange("q (p s) -> q s p", s=PLACES),
+                    in1=slope[:].rearrange("q (p s) -> q s p", s=PLACES),
+                    op=ALU.mult,
+                )
+                for s0 in range(0, PLACES, SIDE):
+                    turned = turn_pool.tile([P, SIDE, P], BF16)
+                    for i in range(SIDE):
+                        nc.tensor.transpose(turned[:, i, :], dz[:, s0 + i, :], ident[:])
+                    nc.scalar.copy(out=grouped[:, s0 : s0 + SIDE, r, :], in_=turned[:])
+
+            dz_codes = work_pool.tile([P, PLACES, P], U32, align_bytes=64)
+            dz_scales = work_pool.tile([P, PLACES, P], U8, align_bytes=64)
+            for s0, s1 in ((0, PLACES - 1), (PLACES - 1, PLACES)):
+                nc.vector.quantize_mx(
+                    out=dz_codes[:, s0:s1, :].rearrange("p s m -> p (s m)").bitcast(E5M2X4),
+                    scales=dz_scales[:, s0:s1, :].rearrange("p s m -> p (s m)"),
+                    in_=grouped[:, s0:s1, :, :].rearrange("p s r q -> p (s r q)"),
+                )
+
+            result = work_pool.tile([P, C * PLACES], F32)
+            for a in range(SIDE):
+                acc = acc_pool.tile([P, N_COLS], F32)
+                row_passes = [k for k in range(len(passes)) if passes[k][2] == a]
+                for k in row_passes:
+                    place = SIDE * passes[k][0] + passes[k][1]
+                    nc.tensor.matmul_mx(
+                        out=acc[:],
+                        lhsT=dz_codes[:, place, :].bitcast(E5M2X4),
+                        lhsT_scale=dz_scales[:, place, :],
+                        rhs=w_codes[:, k, :, :, :].rearrange("p f b c -> p (f b c)").bitcast(E4M3X4),
+                        rhs_scale=w_scales[:, k, :, :, :].rearrange("p f b c -> p (f b c)"),
+                        start=(k == row_passes[0]),
+                        stop=(k == row_passes[-1]),
+                    )
+                nc.scalar.copy(
+                    out=result[:].rearrange("n (f c a b) -> n f c a b", f=PARTS, a=SIDE, b=SIDE)[:, :, :, a, :],
+                    in_=acc[:].rearrange("n (f b c) -> n f c b", f=PARTS, b=SLOTS)[:, :, :, 0:SIDE],
+                )
+            nc.scalar.dma_start(out=out_rows[block * P : (block + 1) * P, :], in_=result[:])

@@ -118,9 +118,9 @@ def tile_locallyconnected2d_t_v_kernel(tc, x, weight, bias, z, grad_out, out):
                 )
                 dz = dz_pool.tile([P, PLACES, P], BF16)
                 nc.vector.tensor_tensor(
-                    out=dz[:],
-                    in0=g_t[:].rearrange("q (p s) -> q s p", s=PLACES),
-                    in1=slope[:].rearrange("q (p s) -> q s p", s=PLACES),
+                    out=dz[:].rearrange("q (h w) p -> q h p w", w=SIDE),
+                    in0=g_t[:].rearrange("q (p h w) -> q h p w", h=SIDE, w=SIDE),
+                    in1=slope[:].rearrange("q (p h w) -> q h p w", h=SIDE, w=SIDE),
                     op=ALU.mult,
                 )
                 for s0 in range(0, PLACES, SIDE):

@@ -75,7 +75,7 @@ def tile_locallyconnected2d_t_v_kernel(tc, x, weight, bias, z, grad_out, out):
                     first = (SIDE * h + w) * TAPS + SIDE * (a - h + 1) + (cols[0] - w + 1)
                     src = raw[:, :, :, first : first + len(cols)]
                     dst = stage[:, slot : slot + len(cols), c_lo : c_lo + C_LOAD, :]
-                    if w == 1:
+                    if w > 0:
                         nc.vector.tensor_copy(
                             out=dst.rearrange("p b c j -> p c b j"),
                             in_=src.rearrange("p j c b -> p c b j"),

@@ -11,6 +11,7 @@ I32 = mybir.dt.int32
 E4M3X4 = mybir.dt.float8_e4m3fn_x4
 E5M2X4 = mybir.dt.float8_e5m2_x4
 ALU = mybir.AluOpType
+ACT = mybir.ActivationFunctionType
 
 P = 128
 PACK = 4
@@ -19,6 +20,8 @@ SIDE = 3
 PLACES = SIDE * SIDE
 TAPS = SIDE * SIDE
 NEG_SLOPE = 0.1
+SIGN_SCALE = 2.0**100
+SIGN_BIAS = 2.0**-60
 
 SLOTS = 4
 C_PART = 64
@@ -112,17 +115,18 @@ def tile_locallyconnected2d_t_v_kernel(tc, x, weight, bias, z, grad_out, out):
                 g_t = load_pool.tile([P, P * PLACES], BF16)
                 nc.sync.dma_start(out=g_t[:], in_=g_rows[row0 : row0 + P, :])
 
-                slope = work_pool.tile([P, P * PLACES], F32)
-                nc.vector.tensor_scalar(
-                    out=slope[:], in0=z_t[:], scalar1=0.0, scalar2=NEG_SLOPE, op0=ALU.is_ge, op1=ALU.max
-                )
+                sgn = work_pool.tile([P, P * PLACES], BF16)
+                nc.scalar.activation(out=sgn[:], in_=z_t[:], func=ACT.Sign, scale=SIGN_SCALE, bias=SIGN_BIAS)
                 dz = dz_pool.tile([P, PLACES, P], BF16)
-                nc.vector.tensor_tensor(
-                    out=dz[:].rearrange("q (h w) p -> q h p w", w=SIDE),
-                    in0=g_t[:].rearrange("q (p h w) -> q h p w", h=SIDE, w=SIDE),
-                    in1=slope[:].rearrange("q (p h w) -> q h p w", h=SIDE, w=SIDE),
-                    op=ALU.mult,
-                )
+                for h in range(SIDE):
+                    nc.vector.scalar_tensor_tensor(
+                        out=dz[:, SIDE * h : SIDE * (h + 1), :].rearrange("q w p -> q p w"),
+                        in0=sgn[:].rearrange("q (p h w) -> q h p w", h=SIDE, w=SIDE)[:, h, :, :],
+                        scalar=NEG_SLOPE,
+                        in1=g_t[:].rearrange("q (p h w) -> q h p w", h=SIDE, w=SIDE)[:, h, :, :],
+                        op0=ALU.max,
+                        op1=ALU.mult,
+                    )
                 for s0 in range(0, PLACES, SIDE):
                     turned = turn_pool.tile([P, SIDE, P], BF16)
                     for i in range(SIDE):

@@ -142,7 +142,7 @@ def tile_locallyconnected2d_t_v_kernel(tc, x, weight, bias, z, grad_out, out):
                     in_=grouped[:, s0:s1, :, :].rearrange("p s r q -> p (s r q)"),
                 )
 
-            result = work_pool.tile([P, C * PLACES], F32)
+            padded = work_pool.tile([P, C, SIDE, SLOTS], F32)
             for a in range(SIDE):
                 acc = acc_pool.tile([P, N_COLS], F32)
                 row_passes = [k for k in range(len(passes)) if passes[k][2] == a]
@@ -158,7 +158,12 @@ def tile_locallyconnected2d_t_v_kernel(tc, x, weight, bias, z, grad_out, out):
                         stop=(k == row_passes[-1]),
                     )
                 nc.scalar.copy(
-                    out=result[:].rearrange("n (f c a b) -> n f c a b", f=PARTS, a=SIDE, b=SIDE)[:, :, :, a, :],
-                    in_=acc[:].rearrange("n (f b c) -> n f c b", f=PARTS, b=SLOTS)[:, :, :, 0:SIDE],
+                    out=padded[:].rearrange("n (f c) a b -> n f c a b", f=PARTS)[:, :, :, a, :],
+                    in_=acc[:].rearrange("n (f b c) -> n f c b", f=PARTS, b=SLOTS),
                 )
-            nc.scalar.dma_start(out=out_rows[block * P : (block + 1) * P, :], in_=result[:])
+            result = work_pool.tile([P, C * PLACES], F32)
+            nc.vector.tensor_copy(
+                out=result[:].rearrange("n (g b) -> n g b", b=SIDE),
+                in_=padded[:].rearrange("n c a b -> n (c a) b")[:, :, 0:SIDE],
+            )
+            nc.sync.dma_start(out=out_rows[block * P : (block + 1) * P, :], in_=result[:])

@@ -23,13 +23,27 @@ NEG_SLOPE = 0.1
 SIGN_SCALE = 2.0**100
 SIGN_BIAS = 2.0**-60
 
+HALVES = 2
+PAIR = 2
+O_HALF = O // HALVES
+WORDS = O_HALF // PAIR
+CHUNK = P // HALVES
+CHUNKS = N // CHUNK
+BLOCK_CHUNKS = P // CHUNK
+PIECES = 2
+O_PIECE = O_HALF // PIECES
+PIECE_COLS = O_PIECE * PLACES
+CHUNK_COLS = O_HALF * PLACES
+
 SLOTS = 4
 C_PART = 64
 PARTS = C // C_PART
 C_LOAD = 32
+W_LOADS = C // C_LOAD
 N_COLS = PARTS * SLOTS * C_PART
 
 USED_TAPS = 49
+ROW_TAPS = (14, 21, 14)
 FLOPS = 2 * USED_TAPS * N * O * C
 BYTES = USED_TAPS * O * C * 2 + N * O * PLACES * (4 + 2) + N * C * PLACES * 4
 
@@ -41,97 +55,84 @@ def near(v):
 def tile_locallyconnected2d_t_v_kernel(tc, x, weight, bias, z, grad_out, out):
     nc = tc.nc
 
-    w_rows = weight.rearrange("u (j p) c h w t -> p (u j) c (h w t)", p=P)
-    z_rows = z.rearrange("n (j p) h w -> (n j) (p h w)", j=PACK)
-    g_rows = grad_out.rearrange("n (j p) h w -> (n j) (p h w)", j=PACK)
+    w_rows = weight.rearrange("one (u p e) c h w t -> p (one u) e c (h w t)", u=HALVES, e=PAIR)
+    z_rows = z.rearrange("n (u q) h w -> (n u) (q h w)", u=HALVES)
+    g_rows = grad_out.rearrange("n (u q) h w -> (n u) (q h w)", u=HALVES)
     out_rows = out.rearrange("n c a b -> n (c a b)")
 
     passes = [(h, w, a) for a in range(SIDE) for h in near(a) for w in range(SIDE)]
 
     with ExitStack() as ctx:
         keep = ctx.enter_context(tc.tile_pool(name="keep", bufs=1))
-        w_raw_pool = ctx.enter_context(tc.tile_pool(name="w_raw", bufs=3))
+        big_pool = ctx.enter_context(tc.tile_pool(name="big", bufs=4))
         w_stage_pool = ctx.enter_context(tc.tile_pool(name="w_stage", bufs=1))
-        load_pool = ctx.enter_context(tc.tile_pool(name="load", bufs=5))
-        work_pool = ctx.enter_context(tc.tile_pool(name="work", bufs=2))
+        sgn_pool = ctx.enter_context(tc.tile_pool(name="sgn", bufs=3))
         dz_pool = ctx.enter_context(tc.tile_pool(name="dz", bufs=3))
-        turn_pool = ctx.enter_context(tc.psum_pool(name="turn", bufs=3))
-        acc_pool = ctx.enter_context(tc.psum_pool(name="acc", bufs=5))
+        work_pool = ctx.enter_context(tc.tile_pool(name="work", bufs=2))
+        turn_pool = ctx.enter_context(tc.psum_pool(name="turn", bufs=4))
+        acc_pool = ctx.enter_context(tc.psum_pool(name="acc", bufs=4))
 
-        ident = keep.tile([P, P], BF16)
+        def load_chunk(chunk):
+            both = big_pool.tile([P, CHUNK_COLS + CHUNK_COLS // PAIR], F32, tag="big")
+            z_t = both[:, 0:CHUNK_COLS]
+            g_t = both[:, CHUNK_COLS:].bitcast(BF16)
+            rows = slice(chunk * P, (chunk + 1) * P)
+            for piece in range(PIECES):
+                cols = slice(piece * PIECE_COLS, (piece + 1) * PIECE_COLS)
+                nc.sync.dma_start(out=z_t[:, cols], in_=z_rows[rows, cols])
+                nc.sync.dma_start(out=g_t[:, cols], in_=g_rows[rows, cols])
+            return z_t, g_t
+
+        def load_weights(k):
+            raw = big_pool.tile([P, PACK, C_LOAD, PLACES * TAPS], BF16, tag="big")
+            for u in range(HALVES):
+                nc.sync.dma_start(
+                    out=raw[:, PAIR * u : PAIR * (u + 1), :, :],
+                    in_=w_rows[:, u, :, k * C_LOAD : (k + 1) * C_LOAD, :],
+                )
+            return raw
+
+        loaded = [load_chunk(chunk) for chunk in range(BLOCK_CHUNKS)]
+        raws = [load_weights(k) for k in range(W_LOADS)]
+        loaded.extend([load_chunk(chunk) for chunk in range(BLOCK_CHUNKS, CHUNKS)])
+
+        ident = keep.tile([P, P], F32)
         make_identity(nc, ident[:])
 
         w_codes = keep.tile([P, len(passes), PARTS, SLOTS, C_PART], U32, align_bytes=64)
         w_scales = keep.tile([P, len(passes), PARTS, SLOTS, C_PART], U8, align_bytes=64)
-        nc.vector.memset(w_codes[:].bitcast(I32), 0)
-        nc.vector.memset(w_scales[:].bitcast(I32), 0)
+        for plane in (w_codes, w_scales):
+            nc.vector.memset(plane[:, :, :, SLOTS - 1, :].bitcast(I32), 0)
+            nc.vector.memset(plane[:, 0::SIDE, :, 2, :].bitcast(I32), 0)
+            nc.vector.memset(plane[:, 2::SIDE, :, 0, :].bitcast(I32), 0)
 
-        for part in range(PARTS):
-            stage = w_stage_pool.tile([P, USED_TAPS, C_PART, PACK], BF16, align_bytes=64)
-            for c_lo in range(0, C_PART, C_LOAD):
-                raw = w_raw_pool.tile([P, PACK, C_LOAD, PLACES * TAPS], BF16)
-                c0 = part * C_PART + c_lo
-                nc.sync.dma_start(out=raw[:], in_=w_rows[:, :, c0 : c0 + C_LOAD, :])
-                slot = 0
-                for h, w, a in passes:
-                    cols = near(w)
-                    first = (SIDE * h + w) * TAPS + SIDE * (a - h + 1) + (cols[0] - w + 1)
-                    src = raw[:, :, :, first : first + len(cols)]
-                    dst = stage[:, slot : slot + len(cols), c_lo : c_lo + C_LOAD, :]
-                    if w > 0:
-                        nc.vector.tensor_copy(
-                            out=dst.rearrange("p b c j -> p c b j"),
-                            in_=src.rearrange("p j c b -> p c b j"),
-                        )
-                    else:
-                        nc.scalar.copy(
-                            out=dst.rearrange("p b c j -> p c b j"),
-                            in_=src.rearrange("p j c b -> p c b j"),
-                        )
-                    slot += len(cols)
-            slot = 0
-            for k, (h, w, a) in enumerate(passes):
-                cols = near(w)
-                for s in range(0, len(cols), 2):
-                    n_slots = min(2, len(cols) - s)
-                    b = cols[0] + s
-                    nc.vector.quantize_mx(
-                        out=w_codes[:, k, part, b : b + n_slots, :]
-                        .rearrange("p b c -> p (b c)")
-                        .bitcast(E4M3X4),
-                        scales=w_scales[:, k, part, b : b + n_slots, :].rearrange("p b c -> p (b c)"),
-                        in_=stage[:, slot + s : slot + s + n_slots, :, :].rearrange(
-                            "p b c j -> p (b c j)"
-                        ),
+        def prepare(block):
+            grouped = work_pool.tile([P, PLACES, BLOCK_CHUNKS, PACK * CHUNK], BF16, align_bytes=64)
+            for r in range(BLOCK_CHUNKS):
+                z_t, g_t = loaded[block * BLOCK_CHUNKS + r]
+                dz = dz_pool.tile([P, PLACES, O_HALF], BF16)
+                for piece in range(PIECES):
+                    cols = slice(piece * PIECE_COLS, (piece + 1) * PIECE_COLS)
+                    sgn = sgn_pool.tile([P, PIECE_COLS], BF16)
+                    nc.scalar.activation(
+                        out=sgn[:], in_=z_t[:, cols], func=ACT.Sign, scale=SIGN_SCALE, bias=SIGN_BIAS
                     )
-                slot += len(cols)
-
-        for block in range(N // P):
-            grouped = work_pool.tile([P, PLACES, PACK, P], BF16, align_bytes=64)
-            for r in range(PACK):
-                row0 = (block * PACK + r) * P
-                z_t = load_pool.tile([P, P * PLACES], F32)
-                nc.sync.dma_start(out=z_t[:], in_=z_rows[row0 : row0 + P, :])
-                g_t = load_pool.tile([P, P * PLACES], BF16)
-                nc.sync.dma_start(out=g_t[:], in_=g_rows[row0 : row0 + P, :])
-
-                sgn = work_pool.tile([P, P * PLACES], BF16)
-                nc.scalar.activation(out=sgn[:], in_=z_t[:], func=ACT.Sign, scale=SIGN_SCALE, bias=SIGN_BIAS)
-                dz = dz_pool.tile([P, PLACES, P], BF16)
-                for h in range(SIDE):
-                    nc.vector.scalar_tensor_tensor(
-                        out=dz[:, SIDE * h : SIDE * (h + 1), :].rearrange("q w p -> q p w"),
-                        in0=sgn[:].rearrange("q (p h w) -> q h p w", h=SIDE, w=SIDE)[:, h, :, :],
-                        scalar=NEG_SLOPE,
-                        in1=g_t[:].rearrange("q (p h w) -> q h p w", h=SIDE, w=SIDE)[:, h, :, :],
-                        op0=ALU.max,
-                        op1=ALU.mult,
-                    )
+                    for h in range(SIDE):
+                        nc.vector.scalar_tensor_tensor(
+                            out=dz[
+                                :, SIDE * h : SIDE * (h + 1), piece * O_PIECE : (piece + 1) * O_PIECE
+                            ].rearrange("q w p -> q p w"),
+                            in0=sgn[:].rearrange("q (p h w) -> q h p w", h=SIDE, w=SIDE)[:, h, :, :],
+                            scalar=NEG_SLOPE,
+                            in1=g_t[:, cols].rearrange("q (p h w) -> q h p w", h=SIDE, w=SIDE)[:, h, :, :],
+                            op0=ALU.max,
+                            op1=ALU.mult,
+                        )
                 for s0 in range(0, PLACES, SIDE):
-                    turned = turn_pool.tile([P, SIDE, P], BF16)
+                    turned = turn_pool.tile([P, SIDE, P], F32)
                     for i in range(SIDE):
-                        nc.tensor.transpose(turned[:, i, :], dz[:, s0 + i, :], ident[:])
-                    nc.scalar.copy(out=grouped[:, s0 : s0 + SIDE, r, :], in_=turned[:])
+                        nc.tensor.transpose(turned[:, i, :], dz[:, s0 + i, :].bitcast(F32), ident[:])
+                    nc.scalar.copy(out=grouped[:].bitcast(F32)[:, s0 : s0 + SIDE, r, :], in_=turned[:])
 
             dz_codes = work_pool.tile([P, PLACES, P], U32, align_bytes=64)
             dz_scales = work_pool.tile([P, PLACES, P], U8, align_bytes=64)
@@ -141,7 +142,9 @@ def tile_locallyconnected2d_t_v_kernel(tc, x, weight, bias, z, grad_out, out):
                     scales=dz_scales[:, s0:s1, :].rearrange("p s m -> p (s m)"),
                     in_=grouped[:, s0:s1, :, :].rearrange("p s r q -> p (s r q)"),
                 )
+            return dz_codes, dz_scales
 
+        def multiply(block, dz_codes, dz_scales):
             padded = work_pool.tile([P, C, SIDE, SLOTS], F32)
             for a in range(SIDE):
                 acc = acc_pool.tile([P, N_COLS], F32)
@@ -167,3 +170,52 @@ def tile_locallyconnected2d_t_v_kernel(tc, x, weight, bias, z, grad_out, out):
                 in_=padded[:].rearrange("n c a b -> n (c a) b")[:, :, 0:SIDE],
             )
             nc.sync.dma_start(out=out_rows[block * P : (block + 1) * P, :], in_=result[:])
+
+        ready = prepare(0)
+
+        for part in range(PARTS):
+            stages = [
+                w_stage_pool.tile([P, ROW_TAPS[a], C_PART, PACK], BF16, align_bytes=64, name="stage%d" % a)
+                for a in range(SIDE)
+            ]
+            for c_lo in range(0, C_PART, C_LOAD):
+                raw = raws[(part * C_PART + c_lo) // C_LOAD]
+                slot = [0, 0, 0]
+                for h, w, a in passes:
+                    cols = near(w)
+                    tap0 = (SIDE * h + w) * TAPS + SIDE * (a - h + 1) + (cols[0] - w + 1)
+                    src = raw[:, :, :, tap0 : tap0 + len(cols)]
+                    dst = stages[a][:, slot[a] : slot[a] + len(cols), c_lo : c_lo + C_LOAD, :]
+                    if w == 1:
+                        nc.vector.tensor_copy(
+                            out=dst.rearrange("p b c j -> p c b j"),
+                            in_=src.rearrange("p j c b -> p c b j"),
+                        )
+                    else:
+                        nc.scalar.copy(
+                            out=dst.rearrange("p b c j -> p c b j"),
+                            in_=src.rearrange("p j c b -> p c b j"),
+                        )
+                    slot[a] += len(cols)
+            slot = [0, 0, 0]
+            for k, (h, w, a) in enumerate(passes):
+                cols = near(w)
+                for s in range(0, len(cols), 2):
+                    n_slots = min(2, len(cols) - s)
+                    b = cols[0] + s
+                    nc.vector.quantize_mx(
+                        out=w_codes[:, k, part, b : b + n_slots, :]
+                        .rearrange("p b c -> p (b c)")
+                        .bitcast(E4M3X4),
+                        scales=w_scales[:, k, part, b : b + n_slots, :].rearrange("p b c -> p (b c)"),
+                        in_=stages[a][:, slot[a] + s : slot[a] + s + n_slots, :, :].rearrange(
+                            "p b c j -> p (b c j)"
+                        ),
+                    )
+                slot[a] += len(cols)
+
+        for block in range(1, N // P):
+            following = prepare(block)
+            multiply(block - 1, ready[0], ready[1])
+            ready = following
+        multiply(N // P - 1, ready[0], ready[1])

@@ -108,15 +108,22 @@ def tile_locallyconnected2d_t_v_kernel(tc, x, weight, bias, z, grad_out, out):
 
         def prepare(block):
             grouped = work_pool.tile([P, PLACES, BLOCK_CHUNKS, PACK * CHUNK], BF16, align_bytes=64)
+            dz_codes = work_pool.tile([P, PLACES, P], U32, align_bytes=64)
+            dz_scales = work_pool.tile([P, PLACES, P], U8, align_bytes=64)
             for r in range(BLOCK_CHUNKS):
                 z_t, g_t = loaded[block * BLOCK_CHUNKS + r]
                 dz = dz_pool.tile([P, PLACES, O_HALF], BF16)
                 for piece in range(PIECES):
                     cols = slice(piece * PIECE_COLS, (piece + 1) * PIECE_COLS)
                     sgn = sgn_pool.tile([P, PIECE_COLS], BF16)
-                    nc.scalar.activation(
-                        out=sgn[:], in_=z_t[:, cols], func=ACT.Sign, scale=SIGN_SCALE, bias=SIGN_BIAS
-                    )
+                    if r == BLOCK_CHUNKS - 1 and piece == PIECES - 1:
+                        nc.vector.tensor_scalar(
+                            out=sgn[:], in0=z_t[:, cols], scalar1=0.0, scalar2=None, op0=ALU.is_ge
+                        )
+                    else:
+                        nc.scalar.activation(
+                            out=sgn[:], in_=z_t[:, cols], func=ACT.Sign, scale=SIGN_SCALE, bias=SIGN_BIAS
+                        )
                     for h in range(SIDE):
                         nc.vector.scalar_tensor_tensor(
                             out=dz[
@@ -133,15 +140,14 @@ def tile_locallyconnected2d_t_v_kernel(tc, x, weight, bias, z, grad_out, out):
                     for i in range(SIDE):
                         nc.tensor.transpose(turned[:, i, :], dz[:, s0 + i, :].bitcast(F32), ident[:])
                     nc.scalar.copy(out=grouped[:].bitcast(F32)[:, s0 : s0 + SIDE, r, :], in_=turned[:])
-
-            dz_codes = work_pool.tile([P, PLACES, P], U32, align_bytes=64)
-            dz_scales = work_pool.tile([P, PLACES, P], U8, align_bytes=64)
-            for s0, s1 in ((0, PLACES - 1), (PLACES - 1, PLACES)):
-                nc.vector.quantize_mx(
-                    out=dz_codes[:, s0:s1, :].rearrange("p s m -> p (s m)").bitcast(E5M2X4),
-                    scales=dz_scales[:, s0:s1, :].rearrange("p s m -> p (s m)"),
-                    in_=grouped[:, s0:s1, :, :].rearrange("p s r q -> p (s r q)"),
-                )
+                    if r < BLOCK_CHUNKS - 1:
+                        continue
+                    for q0, q1 in ((s0, s0 + 2), (s0 + 2, s0 + SIDE)):
+                        nc.vector.quantize_mx(
+                            out=dz_codes[:, q0:q1, :].rearrange("p s m -> p (s m)").bitcast(E5M2X4),
+                            scales=dz_scales[:, q0:q1, :].rearrange("p s m -> p (s m)"),
+                            in_=grouped[:, q0:q1, :, :].rearrange("p s r q -> p (s r q)"),
+                        )
             return dz_codes, dz_scales
 
         def multiply(block, dz_codes, dz_scales):

@@ -66,7 +66,7 @@ def tile_locallyconnected2d_t_v_kernel(tc, x, weight, bias, z, grad_out, out):
         keep = ctx.enter_context(tc.tile_pool(name="keep", bufs=1))
         big_pool = ctx.enter_context(tc.tile_pool(name="big", bufs=4))
         w_stage_pool = ctx.enter_context(tc.tile_pool(name="w_stage", bufs=1))
-        sgn_pool = ctx.enter_context(tc.tile_pool(name="sgn", bufs=3))
+        sgn_pool = ctx.enter_context(tc.tile_pool(name="sgn", bufs=4))
         dz_pool = ctx.enter_context(tc.tile_pool(name="dz", bufs=3))
         work_pool = ctx.enter_context(tc.tile_pool(name="work", bufs=2))
         turn_pool = ctx.enter_context(tc.psum_pool(name="turn", bufs=4))
@@ -106,76 +106,135 @@ def tile_locallyconnected2d_t_v_kernel(tc, x, weight, bias, z, grad_out, out):
             nc.vector.memset(plane[:, 0::SIDE, :, 2, :].bitcast(I32), 0)
             nc.vector.memset(plane[:, 2::SIDE, :, 0, :].bitcast(I32), 0)
 
-        def prepare(block):
-            grouped = work_pool.tile([P, PLACES, BLOCK_CHUNKS, PACK * CHUNK], BF16, align_bytes=64)
-            dz_codes = work_pool.tile([P, PLACES, P], U32, align_bytes=64)
-            dz_scales = work_pool.tile([P, PLACES, P], U8, align_bytes=64)
-            for r in range(BLOCK_CHUNKS):
-                z_t, g_t = loaded[block * BLOCK_CHUNKS + r]
-                dz = dz_pool.tile([P, PLACES, O_HALF], BF16)
-                for piece in range(PIECES):
-                    cols = slice(piece * PIECE_COLS, (piece + 1) * PIECE_COLS)
-                    sgn = sgn_pool.tile([P, PIECE_COLS], BF16)
-                    if r == BLOCK_CHUNKS - 1 and piece == PIECES - 1:
-                        nc.vector.tensor_scalar(
-                            out=sgn[:], in0=z_t[:, cols], scalar1=0.0, scalar2=None, op0=ALU.is_ge
-                        )
-                    else:
-                        nc.scalar.activation(
-                            out=sgn[:], in_=z_t[:, cols], func=ACT.Sign, scale=SIGN_SCALE, bias=SIGN_BIAS
-                        )
-                    for h in range(SIDE):
-                        nc.vector.scalar_tensor_tensor(
-                            out=dz[
-                                :, SIDE * h : SIDE * (h + 1), piece * O_PIECE : (piece + 1) * O_PIECE
-                            ].rearrange("q w p -> q p w"),
-                            in0=sgn[:].rearrange("q (p h w) -> q h p w", h=SIDE, w=SIDE)[:, h, :, :],
-                            scalar=NEG_SLOPE,
-                            in1=g_t[:, cols].rearrange("q (p h w) -> q h p w", h=SIDE, w=SIDE)[:, h, :, :],
-                            op0=ALU.max,
-                            op1=ALU.mult,
-                        )
-                for s0 in range(0, PLACES, SIDE):
-                    turned = turn_pool.tile([P, SIDE, P], F32)
-                    for i in range(SIDE):
-                        nc.tensor.transpose(turned[:, i, :], dz[:, s0 + i, :].bitcast(F32), ident[:])
-                    nc.scalar.copy(out=grouped[:].bitcast(F32)[:, s0 : s0 + SIDE, r, :], in_=turned[:])
-                    if r < BLOCK_CHUNKS - 1:
-                        continue
-                    for q0, q1 in ((s0, s0 + 2), (s0 + 2, s0 + SIDE)):
-                        nc.vector.quantize_mx(
-                            out=dz_codes[:, q0:q1, :].rearrange("p s m -> p (s m)").bitcast(E5M2X4),
-                            scales=dz_scales[:, q0:q1, :].rearrange("p s m -> p (s m)"),
-                            in_=grouped[:, q0:q1, :, :].rearrange("p s r q -> p (s r q)"),
-                        )
-            return dz_codes, dz_scales
-
-        def multiply(block, dz_codes, dz_scales):
-            padded = work_pool.tile([P, C, SIDE, SLOTS], F32)
-            for a in range(SIDE):
-                acc = acc_pool.tile([P, N_COLS], F32)
-                row_passes = [k for k in range(len(passes)) if passes[k][2] == a]
-                for k in row_passes:
-                    place = SIDE * passes[k][0] + passes[k][1]
-                    nc.tensor.matmul_mx(
-                        out=acc[:],
-                        lhsT=dz_codes[:, place, :].bitcast(E5M2X4),
-                        lhsT_scale=dz_scales[:, place, :],
-                        rhs=w_codes[:, k, :, :, :].rearrange("p f b c -> p (f b c)").bitcast(E4M3X4),
-                        rhs_scale=w_scales[:, k, :, :, :].rearrange("p f b c -> p (f b c)"),
-                        start=(k == row_passes[0]),
-                        stop=(k == row_passes[-1]),
-                    )
-                nc.scalar.copy(
-                    out=padded[:].rearrange("n (f c) a b -> n f c a b", f=PARTS)[:, :, :, a, :],
-                    in_=acc[:].rearrange("n (f b c) -> n f c b", f=PARTS, b=SLOTS),
+        def make_sign(chunk, piece, on_vector):
+            z_t = loaded[chunk][0]
+            cols = slice(piece * PIECE_COLS, (piece + 1) * PIECE_COLS)
+            sgn = sgn_pool.tile([P, PIECE_COLS], BF16)
+            if on_vector:
+                nc.vector.tensor_scalar(out=sgn[:], in0=z_t[:, cols], scalar1=0.0, scalar2=None, op0=ALU.is_ge)
+            else:
+                nc.scalar.activation(
+                    out=sgn[:], in_=z_t[:, cols], func=ACT.Sign, scale=SIGN_SCALE, bias=SIGN_BIAS
                 )
+            return sgn
+
+        def product(chunk, piece, h, sgn, dz):
+            g_t = loaded[chunk][1]
+            cols = slice(piece * PIECE_COLS, (piece + 1) * PIECE_COLS)
+            nc.vector.scalar_tensor_tensor(
+                out=dz[:, SIDE * h : SIDE * (h + 1), piece * O_PIECE : (piece + 1) * O_PIECE].rearrange(
+                    "q w p -> q p w"
+                ),
+                in0=sgn[:].rearrange("q (p h w) -> q h p w", h=SIDE, w=SIDE)[:, h, :, :],
+                scalar=NEG_SLOPE,
+                in1=g_t[:, cols].rearrange("q (p h w) -> q h p w", h=SIDE, w=SIDE)[:, h, :, :],
+                op0=ALU.max,
+                op1=ALU.mult,
+            )
+
+        def turn(dz, h, grouped, r):
+            turned = turn_pool.tile([P, SIDE, P], F32)
+            for i in range(SIDE):
+                nc.tensor.transpose(turned[:, i, :], dz[:, SIDE * h + i, :].bitcast(F32), ident[:])
+            nc.scalar.copy(out=grouped[:].bitcast(F32)[:, SIDE * h : SIDE * (h + 1), r, :], in_=turned[:])
+
+        def quantise(grouped, h, dz_codes, dz_scales):
+            for q0, q1 in ((SIDE * h, SIDE * h + 2), (SIDE * h + 2, SIDE * (h + 1))):
+                nc.vector.quantize_mx(
+                    out=dz_codes[:, q0:q1, :].rearrange("p s m -> p (s m)").bitcast(E5M2X4),
+                    scales=dz_scales[:, q0:q1, :].rearrange("p s m -> p (s m)"),
+                    in_=grouped[:, q0:q1, :, :].rearrange("p s r q -> p (s r q)"),
+                )
+
+        def one_pass(h, w, a, dz_codes, dz_scales, acc):
+            k = passes.index((h, w, a))
+            nc.tensor.matmul_mx(
+                out=acc[:],
+                lhsT=dz_codes[:, SIDE * h + w, :].bitcast(E5M2X4),
+                lhsT_scale=dz_scales[:, SIDE * h + w, :],
+                rhs=w_codes[:, k, :, :, :].rearrange("p f b c -> p (f b c)").bitcast(E4M3X4),
+                rhs_scale=w_scales[:, k, :, :, :].rearrange("p f b c -> p (f b c)"),
+                start=(h == near(a)[0] and w == 0),
+                stop=(h == near(a)[-1] and w == SIDE - 1),
+            )
+
+        def row_out(acc, a, padded):
+            nc.scalar.copy(
+                out=padded[:].rearrange("n (f c) a b -> n f c a b", f=PARTS)[:, :, :, a, :],
+                in_=acc[:].rearrange("n (f b c) -> n f c b", f=PARTS, b=SLOTS),
+            )
+
+        def store(block, padded):
             result = work_pool.tile([P, C * PLACES], F32)
             nc.vector.tensor_copy(
                 out=result[:].rearrange("n (g b) -> n g b", b=SIDE),
                 in_=padded[:].rearrange("n c a b -> n (c a) b")[:, :, 0:SIDE],
             )
             nc.sync.dma_start(out=out_rows[block * P : (block + 1) * P, :], in_=result[:])
+
+        def on_vector(r, piece):
+            return r == BLOCK_CHUNKS - 1 and piece == PIECES - 1
+
+        def prepare(block):
+            grouped = work_pool.tile([P, PLACES, BLOCK_CHUNKS, PACK * CHUNK], BF16, align_bytes=64)
+            dz_codes = work_pool.tile([P, PLACES, P], U32, align_bytes=64)
+            dz_scales = work_pool.tile([P, PLACES, P], U8, align_bytes=64)
+            for r in range(BLOCK_CHUNKS):
+                chunk = block * BLOCK_CHUNKS + r
+                dz = dz_pool.tile([P, PLACES, O_HALF], BF16)
+                for piece in range(PIECES):
+                    sgn = make_sign(chunk, piece, on_vector(r, piece))
+                    for h in range(SIDE):
+                        product(chunk, piece, h, sgn, dz)
+                for h in range(SIDE):
+                    turn(dz, h, grouped, r)
+                    if r == BLOCK_CHUNKS - 1:
+                        quantise(grouped, h, dz_codes, dz_scales)
+            return dz_codes, dz_scales
+
+        def multiply(block, dz_codes, dz_scales):
+            padded = work_pool.tile([P, C, SIDE, SLOTS], F32)
+            for a in range(SIDE):
+                acc = acc_pool.tile([P, N_COLS], F32)
+                for h in near(a):
+                    for w in range(SIDE):
+                        one_pass(h, w, a, dz_codes, dz_scales, acc)
+                row_out(acc, a, padded)
+            store(block, padded)
+
+        def prepare_by_rows(block):
+            grouped = work_pool.tile([P, PLACES, BLOCK_CHUNKS, PACK * CHUNK], BF16, align_bytes=64)
+            dz_codes = work_pool.tile([P, PLACES, P], U32, align_bytes=64)
+            dz_scales = work_pool.tile([P, PLACES, P], U8, align_bytes=64)
+            signs = {}
+            turning = []
+            for r in range(BLOCK_CHUNKS):
+                dz = dz_pool.tile([P, PLACES, O_HALF], BF16)
+                turning.append(dz)
+                for piece in range(PIECES):
+                    signs[r, piece] = make_sign(block * BLOCK_CHUNKS + r, piece, on_vector(r, piece))
+            for h in range(SIDE):
+                for r in range(BLOCK_CHUNKS):
+                    for piece in range(PIECES):
+                        product(block * BLOCK_CHUNKS + r, piece, h, signs[r, piece], turning[r])
+                for r in range(BLOCK_CHUNKS):
+                    turn(turning[r], h, grouped, r)
+                quantise(grouped, h, dz_codes, dz_scales)
+            return dz_codes, dz_scales
+
+        def multiply_by_rows(block, dz_codes, dz_scales):
+            padded = work_pool.tile([P, C, SIDE, SLOTS], F32)
+            gathering = {}
+            for h in range(SIDE):
+                for a in near(h):
+                    if h == near(a)[0]:
+                        acc = acc_pool.tile([P, N_COLS], F32)
+                        gathering[a] = acc
+                    for w in range(SIDE):
+                        one_pass(h, w, a, dz_codes, dz_scales, gathering[a])
+                    if h == near(a)[-1]:
+                        row_out(gathering[a], a, padded)
+            store(block, padded)
 
         ready = prepare(0)
 
@@ -220,8 +279,10 @@ def tile_locallyconnected2d_t_v_kernel(tc, x, weight, bias, z, grad_out, out):
                     )
                 slot[a] += len(cols)
 
-        for block in range(1, N // P):
+        for block in range(1, N // P - 1):
             following = prepare(block)
             multiply(block - 1, ready[0], ready[1])
             ready = following
-        multiply(N // P - 1, ready[0], ready[1])
+        following = prepare_by_rows(N // P - 1)
+        multiply(N // P - 2, ready[0], ready[1])
+        multiply_by_rows(N // P - 1, following[0], following[1])

@@ -251,7 +251,7 @@ def tile_locallyconnected2d_t_v_kernel(tc, x, weight, bias, z, grad_out, out):
                     tap0 = (SIDE * h + w) * TAPS + SIDE * (a - h + 1) + (cols[0] - w + 1)
                     src = raw[:, :, :, tap0 : tap0 + len(cols)]
                     dst = stages[a][:, slot[a] : slot[a] + len(cols), c_lo : c_lo + C_LOAD, :]
-                    if w == 1:
+                    if w > 0:
                         nc.vector.tensor_copy(
                             out=dst.rearrange("p b c j -> p c b j"),
                             in_=src.rearrange("p j c b -> p c b j"),

@@ -43,7 +43,9 @@ W_LOADS = C // C_LOAD
 N_COLS = PARTS * SLOTS * C_PART
 
 USED_TAPS = 49
-ROW_TAPS = (14, 21, 14)
+ROW_TAPS = (10, 15, 10)
+LEFT = ((0, 0), (1, 0), (0, 1), (1, 1), (2, 1), (1, 2), (2, 2))
+BANK_LEFT = 4
 FLOPS = 2 * USED_TAPS * N * O * C
 BYTES = USED_TAPS * O * C * 2 + N * O * PLACES * (4 + 2) + N * C * PLACES * 4
 
@@ -98,6 +100,8 @@ def tile_locallyconnected2d_t_v_kernel(tc, x, weight, bias, z, grad_out, out):
 
         ident = keep.tile([P, P], F32)
         make_identity(nc, ident[:])
+        ident_16 = keep.tile([P, P], BF16)
+        make_identity(nc, ident_16[:])
 
         w_codes = keep.tile([P, len(passes), PARTS, SLOTS, C_PART], U32, align_bytes=64)
         w_scales = keep.tile([P, len(passes), PARTS, SLOTS, C_PART], U8, align_bytes=64)
@@ -195,7 +199,7 @@ def tile_locallyconnected2d_t_v_kernel(tc, x, weight, bias, z, grad_out, out):
         def multiply(block, dz_codes, dz_scales):
             padded = work_pool.tile([P, C, SIDE, SLOTS], F32)
             for a in range(SIDE):
-                acc = acc_pool.tile([P, N_COLS], F32)
+                acc = acc_pool.tile([P, N_COLS], F32, tag="acc")
                 for h in near(a):
                     for w in range(SIDE):
                         one_pass(h, w, a, dz_codes, dz_scales, acc)
@@ -228,7 +232,7 @@ def tile_locallyconnected2d_t_v_kernel(tc, x, weight, bias, z, grad_out, out):
             for h in range(SIDE):
                 for a in near(h):
                     if h == near(a)[0]:
-                        acc = acc_pool.tile([P, N_COLS], F32)
+                        acc = acc_pool.tile([P, N_COLS], F32, tag="acc")
                         gathering[a] = acc
                     for w in range(SIDE):
                         one_pass(h, w, a, dz_codes, dz_scales, gathering[a])
@@ -243,24 +247,39 @@ def tile_locallyconnected2d_t_v_kernel(tc, x, weight, bias, z, grad_out, out):
                 w_stage_pool.tile([P, ROW_TAPS[a], C_PART, PACK], BF16, align_bytes=64, name="stage%d" % a)
                 for a in range(SIDE)
             ]
+            left = w_stage_pool.tile([P, len(LEFT), PAIR, C_PART, PACK], BF16, align_bytes=64)
             for c_lo in range(0, C_PART, C_LOAD):
                 raw = raws[(part * C_PART + c_lo) // C_LOAD]
+                for i0 in range(0, len(LEFT), BANK_LEFT):
+                    group = LEFT[i0 : i0 + BANK_LEFT]
+                    words = acc_pool.tile([P, len(group), PAIR, C_LOAD, PACK], BF16, tag="acc", name="words")
+                    for i, (h, a) in enumerate(group):
+                        tap0 = SIDE * h * TAPS + SIDE * (a - h + 1) + 1
+                        nc.tensor.matmul(
+                            words[:, i, :, :, :],
+                            lhsT=ident_16[:],
+                            rhs=raw[:, :, :, tap0 : tap0 + PAIR].rearrange("p j c b -> p b c j"),
+                            start=True,
+                            stop=True,
+                        )
+                    nc.scalar.copy(
+                        out=left[:, i0 : i0 + len(group), :, c_lo : c_lo + C_LOAD, :].rearrange(
+                            "p i b c j -> p (i b) c j"
+                        ),
+                        in_=words[:].rearrange("p i b c j -> p (i b) c j"),
+                    )
                 slot = [0, 0, 0]
                 for h, w, a in passes:
+                    if w == 0:
+                        continue
                     cols = near(w)
                     tap0 = (SIDE * h + w) * TAPS + SIDE * (a - h + 1) + (cols[0] - w + 1)
                     src = raw[:, :, :, tap0 : tap0 + len(cols)]
                     dst = stages[a][:, slot[a] : slot[a] + len(cols), c_lo : c_lo + C_LOAD, :]
-                    if w > 0:
-                        nc.vector.tensor_copy(
-                            out=dst.rearrange("p b c j -> p c b j"),
-                            in_=src.rearrange("p j c b -> p c b j"),
-                        )
-                    else:
-                        nc.scalar.copy(
-                            out=dst.rearrange("p b c j -> p c b j"),
-                            in_=src.rearrange("p j c b -> p c b j"),
-                        )
+                    nc.vector.tensor_copy(
+                        out=dst.rearrange("p b c j -> p c b j"),
+                        in_=src.rearrange("p j c b -> p c b j"),
+                    )
                     slot[a] += len(cols)
             slot = [0, 0, 0]
             for k, (h, w, a) in enumerate(passes):
@@ -268,16 +287,19 @@ def tile_locallyconnected2d_t_v_kernel(tc, x, weight, bias, z, grad_out, out):
                 for s in range(0, len(cols), 2):
                     n_slots = min(2, len(cols) - s)
                     b = cols[0] + s
+                    if w == 0:
+                        staged = left[:, list(LEFT).index((h, a)), :, :, :]
+                    else:
+                        staged = stages[a][:, slot[a] + s : slot[a] + s + n_slots, :, :]
                     nc.vector.quantize_mx(
                         out=w_codes[:, k, part, b : b + n_slots, :]
                         .rearrange("p b c -> p (b c)")
                         .bitcast(E4M3X4),
                         scales=w_scales[:, k, part, b : b + n_slots, :].rearrange("p b c -> p (b c)"),
-                        in_=stages[a][:, slot[a] + s : slot[a] + s + n_slots, :, :].rearrange(
-                            "p b c j -> p (b c j)"
-                        ),
+                        in_=staged.rearrange("p b c j -> p (b c j)"),
                     )
-                slot[a] += len(cols)
+                if w > 0:
+                    slot[a] += len(cols)
 
         for block in range(1, N // P - 1):
             following = prepare(block)

@@ -35,16 +35,19 @@ O_PIECE = O_HALF // PIECES
 PIECE_COLS = O_PIECE * PLACES
 CHUNK_COLS = O_HALF * PLACES
 
-SLOTS = 4
 C_PART = 64
 PARTS = C // C_PART
+SLOTS = 8
+N_COLS = SLOTS * C_PART
+CORNER = ((1, 1), (1, 2), (2, 1), (2, 2))
+LAST_PLACE = PARTS
+TARGETS = (0, 1, LAST_PLACE)
+PITCH = 12
 C_LOAD = 32
 W_LOADS = C // C_LOAD
-N_COLS = PARTS * SLOTS * C_PART
 
 USED_TAPS = 49
-ROW_TAPS = (10, 15, 10)
-LEFT = ((0, 0), (1, 0), (0, 1), (1, 1), (2, 1), (1, 2), (2, 2))
+LEFT = ((0, 0), (0, 1), (1, 0), (1, 1), (1, 2), (2, 1), (2, 2))
 BANK_LEFT = 4
 FLOPS = 2 * USED_TAPS * N * O * C
 BYTES = USED_TAPS * O * C * 2 + N * O * PLACES * (4 + 2) + N * C * PLACES * 4
@@ -62,7 +65,6 @@ def tile_locallyconnected2d_t_v_kernel(tc, x, weight, bias, z, grad_out, out):
     g_rows = grad_out.rearrange("n (u q) h w -> (n u) (q h w)", u=HALVES)
     out_rows = out.rearrange("n c a b -> n (c a b)")
 
-    passes = [(h, w, a) for a in range(SIDE) for h in near(a) for w in range(SIDE)]
 
     with ExitStack() as ctx:
         keep = ctx.enter_context(tc.tile_pool(name="keep", bufs=1))
@@ -71,6 +73,7 @@ def tile_locallyconnected2d_t_v_kernel(tc, x, weight, bias, z, grad_out, out):
         sgn_pool = ctx.enter_context(tc.tile_pool(name="sgn", bufs=4))
         dz_pool = ctx.enter_context(tc.tile_pool(name="dz", bufs=3))
         work_pool = ctx.enter_context(tc.tile_pool(name="work", bufs=2))
+        code_pool = ctx.enter_context(tc.tile_pool(name="code", bufs=3))
         turn_pool = ctx.enter_context(tc.psum_pool(name="turn", bufs=4))
         acc_pool = ctx.enter_context(tc.psum_pool(name="acc", bufs=4))
 
@@ -94,21 +97,33 @@ def tile_locallyconnected2d_t_v_kernel(tc, x, weight, bias, z, grad_out, out):
                 )
             return raw
 
-        loaded = [load_chunk(chunk) for chunk in range(BLOCK_CHUNKS)]
-        raws = [load_weights(k) for k in range(W_LOADS)]
-        loaded.extend([load_chunk(chunk) for chunk in range(BLOCK_CHUNKS, CHUNKS)])
+        loaded = []
+        raws = []
+        for part in range(PARTS):
+            loaded.extend([load_chunk(part * BLOCK_CHUNKS + r) for r in range(BLOCK_CHUNKS)])
+            raws.extend([load_weights(part * W_LOADS // PARTS + k) for k in range(W_LOADS // PARTS)])
+        loaded.extend([load_chunk(chunk) for chunk in range(PARTS * BLOCK_CHUNKS, CHUNKS)])
 
         ident = keep.tile([P, P], F32)
         make_identity(nc, ident[:])
         ident_16 = keep.tile([P, P], BF16)
         make_identity(nc, ident_16[:])
 
-        w_codes = keep.tile([P, len(passes), PARTS, SLOTS, C_PART], U32, align_bytes=64)
-        w_scales = keep.tile([P, len(passes), PARTS, SLOTS, C_PART], U8, align_bytes=64)
+        corner_cols = len(CORNER) * C
+        w_codes = keep.tile([P, corner_cols + PARTS * PLACES * N_COLS], U32, align_bytes=64)
+        w_scales = keep.tile([P, corner_cols + PARTS * PLACES * N_COLS], U8, align_bytes=64)
+
+        def main_slots(plane):
+            return plane[:, corner_cols:].rearrange(
+                "p (f h w s c) -> p f h w s c", f=PARTS, h=SIDE, w=SIDE, s=SLOTS
+            )
+
         for plane in (w_codes, w_scales):
-            nc.vector.memset(plane[:, :, :, SLOTS - 1, :].bitcast(I32), 0)
-            nc.vector.memset(plane[:, 0::SIDE, :, 2, :].bitcast(I32), 0)
-            nc.vector.memset(plane[:, 2::SIDE, :, 0, :].bitcast(I32), 0)
+            slots = main_slots(plane)
+            nc.vector.memset(slots[:, :, :, 0, 2::SIDE, :].bitcast(I32), 0)
+            nc.vector.memset(slots[:, :, :, 2, 0::SIDE, :].bitcast(I32), 0)
+            nc.vector.memset(slots[:, :, 0, :, 2 * SIDE :, :].bitcast(I32), 0)
+            nc.vector.memset(slots[:, :, 2, :, 0:SIDE, :].bitcast(I32), 0)
 
         def make_sign(chunk, piece, on_vector):
             z_t = loaded[chunk][0]
@@ -150,39 +165,48 @@ def tile_locallyconnected2d_t_v_kernel(tc, x, weight, bias, z, grad_out, out):
                     in_=grouped[:, q0:q1, :, :].rearrange("p s r q -> p (s r q)"),
                 )
 
-        def one_pass(h, w, a, dz_codes, dz_scales, acc):
-            k = passes.index((h, w, a))
+        def one_pass(target, h, w, dz_codes, dz_scales, acc, start, stop):
+            if target == LAST_PLACE:
+                c0 = list(CORNER).index((h, w)) * C
+            else:
+                c0 = corner_cols + ((target * SIDE + h) * SIDE + w) * N_COLS
             nc.tensor.matmul_mx(
                 out=acc[:],
                 lhsT=dz_codes[:, SIDE * h + w, :].bitcast(E5M2X4),
                 lhsT_scale=dz_scales[:, SIDE * h + w, :],
-                rhs=w_codes[:, k, :, :, :].rearrange("p f b c -> p (f b c)").bitcast(E4M3X4),
-                rhs_scale=w_scales[:, k, :, :, :].rearrange("p f b c -> p (f b c)"),
-                start=(h == near(a)[0] and w == 0),
-                stop=(h == near(a)[-1] and w == SIDE - 1),
+                rhs=w_codes[:, c0 : c0 + N_COLS].bitcast(E4M3X4),
+                rhs_scale=w_scales[:, c0 : c0 + N_COLS],
+                start=start,
+                stop=stop,
             )
 
-        def row_out(acc, a, padded):
-            nc.scalar.copy(
-                out=padded[:].rearrange("n (f c) a b -> n f c a b", f=PARTS)[:, :, :, a, :],
-                in_=acc[:].rearrange("n (f b c) -> n f c b", f=PARTS, b=SLOTS),
-            )
+        def reaching(target):
+            return CORNER if target == LAST_PLACE else [(h, w) for h in range(SIDE) for w in range(SIDE)]
+
+        def bank_out(acc, target, padded):
+            if target == LAST_PLACE:
+                nc.scalar.copy(out=padded[:, :, SLOTS:PITCH], in_=acc[:].rearrange("n (s c) -> n c s", c=C))
+            else:
+                nc.scalar.copy(
+                    out=padded[:, target * C_PART : (target + 1) * C_PART, 0:SLOTS],
+                    in_=acc[:].rearrange("n (s c) -> n c s", c=C_PART),
+                )
 
         def store(block, padded):
             result = work_pool.tile([P, C * PLACES], F32)
             nc.vector.tensor_copy(
-                out=result[:].rearrange("n (g b) -> n g b", b=SIDE),
-                in_=padded[:].rearrange("n c a b -> n (c a) b")[:, :, 0:SIDE],
+                out=result[:].rearrange("n (c s) -> n c s", s=PLACES),
+                in_=padded[:, :, 0:PLACES],
             )
             nc.sync.dma_start(out=out_rows[block * P : (block + 1) * P, :], in_=result[:])
 
         def on_vector(r, piece):
-            return r == BLOCK_CHUNKS - 1 and piece == PIECES - 1
+            return False
 
         def prepare(block):
             grouped = work_pool.tile([P, PLACES, BLOCK_CHUNKS, PACK * CHUNK], BF16, align_bytes=64)
-            dz_codes = work_pool.tile([P, PLACES, P], U32, align_bytes=64)
-            dz_scales = work_pool.tile([P, PLACES, P], U8, align_bytes=64)
+            dz_codes = code_pool.tile([P, PLACES, P], U32, align_bytes=64)
+            dz_scales = code_pool.tile([P, PLACES, P], U8, align_bytes=64)
             for r in range(BLOCK_CHUNKS):
                 chunk = block * BLOCK_CHUNKS + r
                 dz = dz_pool.tile([P, PLACES, O_HALF], BF16)
@@ -196,20 +220,18 @@ def tile_locallyconnected2d_t_v_kernel(tc, x, weight, bias, z, grad_out, out):
                         quantise(grouped, h, dz_codes, dz_scales)
             return dz_codes, dz_scales
 
-        def multiply(block, dz_codes, dz_scales):
-            padded = work_pool.tile([P, C, SIDE, SLOTS], F32)
-            for a in range(SIDE):
+        def multiply(targets, dz_codes, dz_scales, padded):
+            for target in targets:
                 acc = acc_pool.tile([P, N_COLS], F32, tag="acc")
-                for h in near(a):
-                    for w in range(SIDE):
-                        one_pass(h, w, a, dz_codes, dz_scales, acc)
-                row_out(acc, a, padded)
-            store(block, padded)
+                places = reaching(target)
+                for i, (h, w) in enumerate(places):
+                    one_pass(target, h, w, dz_codes, dz_scales, acc, i == 0, i == len(places) - 1)
+                bank_out(acc, target, padded)
 
         def prepare_by_rows(block):
             grouped = work_pool.tile([P, PLACES, BLOCK_CHUNKS, PACK * CHUNK], BF16, align_bytes=64)
-            dz_codes = work_pool.tile([P, PLACES, P], U32, align_bytes=64)
-            dz_scales = work_pool.tile([P, PLACES, P], U8, align_bytes=64)
+            dz_codes = code_pool.tile([P, PLACES, P], U32, align_bytes=64)
+            dz_scales = code_pool.tile([P, PLACES, P], U8, align_bytes=64)
             signs = {}
             turning = []
             for r in range(BLOCK_CHUNKS):
@@ -226,27 +248,34 @@ def tile_locallyconnected2d_t_v_kernel(tc, x, weight, bias, z, grad_out, out):
                 quantise(grouped, h, dz_codes, dz_scales)
             return dz_codes, dz_scales
 
-        def multiply_by_rows(block, dz_codes, dz_scales):
-            padded = work_pool.tile([P, C, SIDE, SLOTS], F32)
+        def multiply_by_rows(dz_codes, dz_scales, padded):
             gathering = {}
+            for row in range(SIDE):
+                for target in TARGETS:
+                    places = reaching(target)
+                    here = [(i, h, w) for i, (h, w) in enumerate(places) if h == row]
+                    for i, h, w in here:
+                        if i == 0:
+                            acc = acc_pool.tile([P, N_COLS], F32, tag="acc")
+                            gathering[target] = acc
+                        one_pass(target, h, w, dz_codes, dz_scales, gathering[target], i == 0, i == len(places) - 1)
+                    if row == SIDE - 1:
+                        bank_out(gathering[target], target, padded)
+
+        def quantise_slots(values, codes, scales):
+            nc.vector.quantize_mx(
+                out=codes.rearrange("p s c -> p (s c)").bitcast(E4M3X4),
+                scales=scales.rearrange("p s c -> p (s c)"),
+                in_=values.rearrange("p s x -> p (s x)"),
+            )
+
+        def weights(part):
+            stages = {}
             for h in range(SIDE):
-                for a in near(h):
-                    if h == near(a)[0]:
-                        acc = acc_pool.tile([P, N_COLS], F32, tag="acc")
-                        gathering[a] = acc
-                    for w in range(SIDE):
-                        one_pass(h, w, a, dz_codes, dz_scales, gathering[a])
-                    if h == near(a)[-1]:
-                        row_out(gathering[a], a, padded)
-            store(block, padded)
-
-        ready = prepare(0)
-
-        for part in range(PARTS):
-            stages = [
-                w_stage_pool.tile([P, ROW_TAPS[a], C_PART, PACK], BF16, align_bytes=64, name="stage%d" % a)
-                for a in range(SIDE)
-            ]
+                for w in range(1, SIDE):
+                    stages[h, w] = w_stage_pool.tile(
+                        [P, len(near(h)), len(near(w)), C_PART, PACK], BF16, align_bytes=64, name="stage%d%d" % (h, w)
+                    )
             left = w_stage_pool.tile([P, len(LEFT), PAIR, C_PART, PACK], BF16, align_bytes=64)
             for c_lo in range(0, C_PART, C_LOAD):
                 raw = raws[(part * C_PART + c_lo) // C_LOAD]
@@ -268,43 +297,74 @@ def tile_locallyconnected2d_t_v_kernel(tc, x, weight, bias, z, grad_out, out):
                         ),
                         in_=words[:].rearrange("p i b c j -> p (i b) c j"),
                     )
-                slot = [0, 0, 0]
-                for h, w, a in passes:
+                for h in range(SIDE):
+                    for w in range(1, SIDE):
+                        rows, cols = near(h), near(w)
+                        src = raw[:, :, :, (SIDE * h + w) * TAPS : (SIDE * h + w + 1) * TAPS].rearrange(
+                            "p q c (i j) -> p q c i j", j=SIDE
+                        )[:, :, :, rows[0] - h + 1 : rows[-1] - h + 2, cols[0] - w + 1 : cols[-1] - w + 2]
+                        copy = nc.scalar.copy if w == 2 and h != 1 else nc.vector.tensor_copy
+                        copy(
+                            out=stages[h, w][:, :, :, c_lo : c_lo + C_LOAD, :].rearrange("p i b c q -> p i c b q"),
+                            in_=src.rearrange("p q c i b -> p i c b q"),
+                        )
+            slots = [main_slots(plane)[:, part, :, :, :, :] for plane in (w_codes, w_scales)]
+            corners = [
+                plane[:, 0:corner_cols].rearrange("p (k f c) -> p k f c", f=PARTS, c=C_PART)[:, :, part, :]
+                for plane in (w_codes, w_scales)
+            ]
+            for h in range(SIDE):
+                for w in range(SIDE):
+                    rows, cols = near(h), near(w)
                     if w == 0:
-                        continue
-                    cols = near(w)
-                    tap0 = (SIDE * h + w) * TAPS + SIDE * (a - h + 1) + (cols[0] - w + 1)
-                    src = raw[:, :, :, tap0 : tap0 + len(cols)]
-                    dst = stages[a][:, slot[a] : slot[a] + len(cols), c_lo : c_lo + C_LOAD, :]
-                    nc.vector.tensor_copy(
-                        out=dst.rearrange("p b c j -> p c b j"),
-                        in_=src.rearrange("p j c b -> p c b j"),
-                    )
-                    slot[a] += len(cols)
-            slot = [0, 0, 0]
-            for k, (h, w, a) in enumerate(passes):
-                cols = near(w)
-                for s in range(0, len(cols), 2):
-                    n_slots = min(2, len(cols) - s)
-                    b = cols[0] + s
-                    if w == 0:
-                        staged = left[:, list(LEFT).index((h, a)), :, :, :]
+                        first = list(LEFT).index((h, rows[0]))
+                        staged = left[:, first : first + len(rows), :, :, :]
                     else:
-                        staged = stages[a][:, slot[a] + s : slot[a] + s + n_slots, :, :]
-                    nc.vector.quantize_mx(
-                        out=w_codes[:, k, part, b : b + n_slots, :]
-                        .rearrange("p b c -> p (b c)")
-                        .bitcast(E4M3X4),
-                        scales=w_scales[:, k, part, b : b + n_slots, :].rearrange("p b c -> p (b c)"),
-                        in_=staged.rearrange("p b c j -> p (b c j)"),
-                    )
-                if w > 0:
-                    slot[a] += len(cols)
+                        staged = stages[h, w][:]
+                    staged = staged.rearrange("p i b c j -> p (i b) (c j)")
+                    total = len(rows) * len(cols)
+                    run = total if w == 1 else len(cols)
+                    for i0 in range(0, total, run):
+                        s0 = SIDE * (rows[0] + i0 // len(cols)) + cols[0]
+                        left_over = min(run, SLOTS - s0)
+                        i = i0
+                        for n in (8, 4, 2, 1):
+                            if left_over >= n:
+                                s = s0 + i - i0
+                                quantise_slots(
+                                    staged[:, i : i + n, :],
+                                    slots[0][:, h, w, s : s + n, :],
+                                    slots[1][:, h, w, s : s + n, :],
+                                )
+                                i += n
+                                left_over -= n
+                    if (h, w) in CORNER:
+                        k = list(CORNER).index((h, w))
+                        quantise_slots(
+                            staged[:, total - 1 : total, :], corners[0][:, k : k + 1, :], corners[1][:, k : k + 1, :]
+                        )
 
-        for block in range(1, N // P - 1):
-            following = prepare(block)
-            multiply(block - 1, ready[0], ready[1])
-            ready = following
-        following = prepare_by_rows(N // P - 1)
-        multiply(N // P - 2, ready[0], ready[1])
-        multiply_by_rows(N // P - 1, following[0], following[1])
+        def pad():
+            padded = work_pool.tile([P, C, PITCH], F32)
+            return padded
+
+        codes0 = prepare(0)
+        weights(0)
+        codes1 = prepare(1)
+        pad0 = pad()
+        multiply(TARGETS[:1], codes0[0], codes0[1], pad0)
+        weights(1)
+        pad1 = pad()
+        multiply(TARGETS[:1], codes1[0], codes1[1], pad1)
+        codes2 = prepare(2)
+        multiply(TARGETS[1:], codes0[0], codes0[1], pad0)
+        store(0, pad0)
+        multiply(TARGETS[1:], codes1[0], codes1[1], pad1)
+        store(1, pad1)
+        codes3 = prepare_by_rows(3)
+        pad2 = pad()
+        multiply(TARGETS, codes2[0], codes2[1], pad2)
+        store(2, pad2)
+        pad3 = pad()
+        multiply_by_rows(codes3[0], codes3[1], pad3)
+        store(3, pad3)

@@ -30,9 +30,9 @@ WORDS = O_HALF // PAIR
 CHUNK = P // HALVES
 CHUNKS = N // CHUNK
 BLOCK_CHUNKS = P // CHUNK
-PIECES = 2
-O_PIECE = O_HALF // PIECES
-PIECE_COLS = O_PIECE * PLACES
+HEAD_CUTS = (0, O_HALF // 4, O_HALF // 2, O_HALF)
+CUTS = (0, O_HALF // 2, O_HALF)
+TAIL_CUTS = (0, O_HALF // 2, 3 * O_HALF // 4, O_HALF)
 CHUNK_COLS = O_HALF * PLACES
 
 C_PART = 64
@@ -57,6 +57,11 @@ def near(v):
     return range(max(0, v - 1), min(SIDE, v + 2))
 
 
+def pieces(chunk):
+    cuts = {0: HEAD_CUTS, CHUNKS - 1: TAIL_CUTS}.get(chunk, CUTS)
+    return list(zip(cuts[:-1], cuts[1:]))
+
+
 def tile_locallyconnected2d_t_v_kernel(tc, x, weight, bias, z, grad_out, out):
     nc = tc.nc
 
@@ -77,24 +82,28 @@ def tile_locallyconnected2d_t_v_kernel(tc, x, weight, bias, z, grad_out, out):
         turn_pool = ctx.enter_context(tc.psum_pool(name="turn", bufs=4))
         acc_pool = ctx.enter_context(tc.psum_pool(name="acc", bufs=4))
 
+        def cuts(k):
+            return ((0, C_LOAD // 2), (C_LOAD // 2, C_LOAD)) if k % 2 else ((0, C_LOAD),)
+
         def load_chunk(chunk):
             both = big_pool.tile([P, CHUNK_COLS + CHUNK_COLS // PAIR], F32, tag="big")
             z_t = both[:, 0:CHUNK_COLS]
             g_t = both[:, CHUNK_COLS:].bitcast(BF16)
             rows = slice(chunk * P, (chunk + 1) * P)
-            for piece in range(PIECES):
-                cols = slice(piece * PIECE_COLS, (piece + 1) * PIECE_COLS)
+            for o0, o1 in pieces(chunk):
+                cols = slice(o0 * PLACES, o1 * PLACES)
                 nc.sync.dma_start(out=z_t[:, cols], in_=z_rows[rows, cols])
                 nc.sync.dma_start(out=g_t[:, cols], in_=g_rows[rows, cols])
             return z_t, g_t
 
         def load_weights(k):
             raw = big_pool.tile([P, PACK, C_LOAD, PLACES * TAPS], BF16, tag="big")
-            for u in range(HALVES):
-                nc.sync.dma_start(
-                    out=raw[:, PAIR * u : PAIR * (u + 1), :, :],
-                    in_=w_rows[:, u, :, k * C_LOAD : (k + 1) * C_LOAD, :],
-                )
+            for c0, c1 in cuts(k):
+                for u in range(HALVES):
+                    nc.sync.dma_start(
+                        out=raw[:, PAIR * u : PAIR * (u + 1), c0:c1, :],
+                        in_=w_rows[:, u, :, k * C_LOAD + c0 : k * C_LOAD + c1, :],
+                    )
             return raw
 
         loaded = []
@@ -125,23 +134,24 @@ def tile_locallyconnected2d_t_v_kernel(tc, x, weight, bias, z, grad_out, out):
             nc.vector.memset(slots[:, :, 0, :, 2 * SIDE :, :].bitcast(I32), 0)
             nc.vector.memset(slots[:, :, 2, :, 0:SIDE, :].bitcast(I32), 0)
 
-        def make_sign(chunk, piece, on_vector):
-            z_t = loaded[chunk][0]
-            cols = slice(piece * PIECE_COLS, (piece + 1) * PIECE_COLS)
-            sgn = sgn_pool.tile([P, PIECE_COLS], BF16)
-            if on_vector:
-                nc.vector.tensor_scalar(out=sgn[:], in0=z_t[:, cols], scalar1=0.0, scalar2=None, op0=ALU.is_ge)
-            else:
-                nc.scalar.activation(
-                    out=sgn[:], in_=z_t[:, cols], func=ACT.Sign, scale=SIGN_SCALE, bias=SIGN_BIAS
-                )
+        def make_sign(chunk, piece):
+            o0, o1 = piece
+            sgn = sgn_pool.tile([P, (o1 - o0) * PLACES], BF16)
+            nc.scalar.activation(
+                out=sgn[:],
+                in_=loaded[chunk][0][:, o0 * PLACES : o1 * PLACES],
+                func=ACT.Sign,
+                scale=SIGN_SCALE,
+                bias=SIGN_BIAS,
+            )
             return sgn
 
         def product(chunk, piece, h, sgn, dz):
             g_t = loaded[chunk][1]
-            cols = slice(piece * PIECE_COLS, (piece + 1) * PIECE_COLS)
+            o0, o1 = piece
+            cols = slice(o0 * PLACES, o1 * PLACES)
             nc.vector.scalar_tensor_tensor(
-                out=dz[:, SIDE * h : SIDE * (h + 1), piece * O_PIECE : (piece + 1) * O_PIECE].rearrange(
+                out=dz[:, SIDE * h : SIDE * (h + 1), o0:o1].rearrange(
                     "q w p -> q p w"
                 ),
                 in0=sgn[:].rearrange("q (p h w) -> q h p w", h=SIDE, w=SIDE)[:, h, :, :],
@@ -192,16 +202,15 @@ def tile_locallyconnected2d_t_v_kernel(tc, x, weight, bias, z, grad_out, out):
                     in_=acc[:].rearrange("n (s c) -> n c s", c=C_PART),
                 )
 
-        def store(block, padded):
-            result = work_pool.tile([P, C * PLACES], F32)
+        def store(block, padded, c0=0, c1=C):
+            result = work_pool.tile([P, (c1 - c0) * PLACES], F32)
             nc.vector.tensor_copy(
                 out=result[:].rearrange("n (c s) -> n c s", s=PLACES),
-                in_=padded[:, :, 0:PLACES],
+                in_=padded[:, c0:c1, 0:PLACES],
             )
-            nc.sync.dma_start(out=out_rows[block * P : (block + 1) * P, :], in_=result[:])
-
-        def on_vector(r, piece):
-            return False
+            nc.sync.dma_start(
+                out=out_rows[block * P : (block + 1) * P, c0 * PLACES : c1 * PLACES], in_=result[:]
+            )
 
         def prepare(block):
             grouped = work_pool.tile([P, PLACES, BLOCK_CHUNKS, PACK * CHUNK], BF16, align_bytes=64)
@@ -210,8 +219,8 @@ def tile_locallyconnected2d_t_v_kernel(tc, x, weight, bias, z, grad_out, out):
             for r in range(BLOCK_CHUNKS):
                 chunk = block * BLOCK_CHUNKS + r
                 dz = dz_pool.tile([P, PLACES, O_HALF], BF16)
-                for piece in range(PIECES):
-                    sgn = make_sign(chunk, piece, on_vector(r, piece))
+                for piece in pieces(chunk):
+                    sgn = make_sign(chunk, piece)
                     for h in range(SIDE):
                         product(chunk, piece, h, sgn, dz)
                 for h in range(SIDE):
@@ -237,21 +246,23 @@ def tile_locallyconnected2d_t_v_kernel(tc, x, weight, bias, z, grad_out, out):
             for r in range(BLOCK_CHUNKS):
                 dz = dz_pool.tile([P, PLACES, O_HALF], BF16)
                 turning.append(dz)
-                for piece in range(PIECES):
-                    signs[r, piece] = make_sign(block * BLOCK_CHUNKS + r, piece, on_vector(r, piece))
+                chunk = block * BLOCK_CHUNKS + r
+                for piece in pieces(chunk):
+                    signs[chunk, piece] = make_sign(chunk, piece)
             for h in range(SIDE):
                 for r in range(BLOCK_CHUNKS):
-                    for piece in range(PIECES):
-                        product(block * BLOCK_CHUNKS + r, piece, h, signs[r, piece], turning[r])
+                    chunk = block * BLOCK_CHUNKS + r
+                    for piece in pieces(chunk):
+                        product(chunk, piece, h, signs[chunk, piece], turning[r])
                 for r in range(BLOCK_CHUNKS):
                     turn(turning[r], h, grouped, r)
                 quantise(grouped, h, dz_codes, dz_scales)
             return dz_codes, dz_scales
 
-        def multiply_by_rows(dz_codes, dz_scales, padded):
+        def multiply_by_rows(block, dz_codes, dz_scales, padded):
             gathering = {}
             for row in range(SIDE):
-                for target in TARGETS:
+                for target in (LAST_PLACE, 0, 1):
                     places = reaching(target)
                     here = [(i, h, w) for i, (h, w) in enumerate(places) if h == row]
                     for i, h, w in here:
@@ -261,6 +272,8 @@ def tile_locallyconnected2d_t_v_kernel(tc, x, weight, bias, z, grad_out, out):
                         one_pass(target, h, w, dz_codes, dz_scales, gathering[target], i == 0, i == len(places) - 1)
                     if row == SIDE - 1:
                         bank_out(gathering[target], target, padded)
+                        if target != LAST_PLACE:
+                            store(block, padded, target * C_PART, (target + 1) * C_PART)
 
         def quantise_slots(values, codes, scales):
             nc.vector.quantize_mx(
@@ -277,11 +290,13 @@ def tile_locallyconnected2d_t_v_kernel(tc, x, weight, bias, z, grad_out, out):
                         [P, len(near(h)), len(near(w)), C_PART, PACK], BF16, align_bytes=64, name="stage%d%d" % (h, w)
                     )
             left = w_stage_pool.tile([P, len(LEFT), PAIR, C_PART, PACK], BF16, align_bytes=64)
-            for c_lo in range(0, C_PART, C_LOAD):
-                raw = raws[(part * C_PART + c_lo) // C_LOAD]
+            loads = range(part * C_PART // C_LOAD, (part + 1) * C_PART // C_LOAD)
+            for k, (c0, c1) in [(k, cut) for k in loads for cut in cuts(k)]:
+                raw = raws[k][:, :, c0:c1, :]
+                staged_c = slice(k * C_LOAD % C_PART + c0, k * C_LOAD % C_PART + c1)
                 for i0 in range(0, len(LEFT), BANK_LEFT):
                     group = LEFT[i0 : i0 + BANK_LEFT]
-                    words = acc_pool.tile([P, len(group), PAIR, C_LOAD, PACK], BF16, tag="acc", name="words")
+                    words = acc_pool.tile([P, len(group), PAIR, c1 - c0, PACK], BF16, tag="acc", name="words")
                     for i, (h, a) in enumerate(group):
                         tap0 = SIDE * h * TAPS + SIDE * (a - h + 1) + 1
                         nc.tensor.matmul(
@@ -292,7 +307,7 @@ def tile_locallyconnected2d_t_v_kernel(tc, x, weight, bias, z, grad_out, out):
                             stop=True,
                         )
                     nc.scalar.copy(
-                        out=left[:, i0 : i0 + len(group), :, c_lo : c_lo + C_LOAD, :].rearrange(
+                        out=left[:, i0 : i0 + len(group), :, staged_c, :].rearrange(
                             "p i b c j -> p (i b) c j"
                         ),
                         in_=words[:].rearrange("p i b c j -> p (i b) c j"),
@@ -305,7 +320,7 @@ def tile_locallyconnected2d_t_v_kernel(tc, x, weight, bias, z, grad_out, out):
                         )[:, :, :, rows[0] - h + 1 : rows[-1] - h + 2, cols[0] - w + 1 : cols[-1] - w + 2]
                         copy = nc.scalar.copy if w == 2 and h != 1 else nc.vector.tensor_copy
                         copy(
-                            out=stages[h, w][:, :, :, c_lo : c_lo + C_LOAD, :].rearrange("p i b c q -> p i c b q"),
+                            out=stages[h, w][:, :, :, staged_c, :].rearrange("p i b c q -> p i c b q"),
                             in_=src.rearrange("p q c i b -> p i c b q"),
                         )
             slots = [main_slots(plane)[:, part, :, :, :, :] for plane in (w_codes, w_scales)]
@@ -366,5 +381,4 @@ def tile_locallyconnected2d_t_v_kernel(tc, x, weight, bias, z, grad_out, out):
         multiply(TARGETS, codes2[0], codes2[1], pad2)
         store(2, pad2)
         pad3 = pad()
-        multiply_by_rows(codes3[0], codes3[1], pad3)
-        store(3, pad3)
+        multiply_by_rows(3, codes3[0], codes3[1], pad3)

@@ -90,7 +90,7 @@ def tile_locallyconnected2d_t_v_kernel(tc, x, weight, bias, z, grad_out, out):
             z_t = both[:, 0:CHUNK_COLS]
             g_t = both[:, CHUNK_COLS:].bitcast(BF16)
             rows = slice(chunk * P, (chunk + 1) * P)
-            for o0, o1 in pieces(chunk):
+            for o0, o1 in pieces(chunk) if chunk == 0 or chunk % BLOCK_CHUNKS else [(0, O_HALF)]:
                 cols = slice(o0 * PLACES, o1 * PLACES)
                 nc.sync.dma_start(out=z_t[:, cols], in_=z_rows[rows, cols])
                 nc.sync.dma_start(out=g_t[:, cols], in_=g_rows[rows, cols])

from contextlib import ExitStack

import concourse.mybir as mybir
from concourse.masks import make_identity

F32 = mybir.dt.float32
BF16 = mybir.dt.bfloat16
U32 = mybir.dt.uint32
U8 = mybir.dt.uint8
I32 = mybir.dt.int32
E4M3X4 = mybir.dt.float8_e4m3fn_x4
E5M2X4 = mybir.dt.float8_e5m2_x4
ALU = mybir.AluOpType
ACT = mybir.ActivationFunctionType

P = 128
PACK = 4
N, C, O = 512, 128, 512
SIDE = 3
PLACES = SIDE * SIDE
TAPS = SIDE * SIDE
NEG_SLOPE = 0.1
SIGN_SCALE = 2.0**100
SIGN_BIAS = 2.0**-60

HALVES = 2
PAIR = 2
O_HALF = O // HALVES
WORDS = O_HALF // PAIR
CHUNK = P // HALVES
CHUNKS = N // CHUNK
BLOCK_CHUNKS = P // CHUNK
HEAD_CUTS = (0, O_HALF // 4, O_HALF // 2, O_HALF)
CUTS = (0, O_HALF // 2, O_HALF)
TAIL_CUTS = (0, O_HALF // 2, 3 * O_HALF // 4, O_HALF)
CHUNK_COLS = O_HALF * PLACES

C_PART = 64
PARTS = C // C_PART
SLOTS = 8
N_COLS = SLOTS * C_PART
CORNER = ((1, 1), (1, 2), (2, 1), (2, 2))
LAST_PLACE = PARTS
TARGETS = (0, 1, LAST_PLACE)
PITCH = 12
C_LOAD = 32
W_LOADS = C // C_LOAD

USED_TAPS = 49
LEFT = ((0, 0), (0, 1), (1, 0), (1, 1), (1, 2), (2, 1), (2, 2))
BANK_LEFT = 4
FLOPS = 2 * USED_TAPS * N * O * C
BYTES = USED_TAPS * O * C * 2 + N * O * PLACES * (4 + 2) + N * C * PLACES * 4


def near(v):
    return range(max(0, v - 1), min(SIDE, v + 2))


def pieces(chunk):
    cuts = {0: HEAD_CUTS, CHUNKS - 1: TAIL_CUTS}.get(chunk, CUTS)
    return list(zip(cuts[:-1], cuts[1:]))


def tile_locallyconnected2d_t_v_kernel(tc, x, weight, bias, z, grad_out, out):
    nc = tc.nc

    w_rows = weight.rearrange("one (u p e) c h w t -> p (one u) e c (h w t)", u=HALVES, e=PAIR)
    z_rows = z.rearrange("n (u q) h w -> (n u) (q h w)", u=HALVES)
    g_rows = grad_out.rearrange("n (u q) h w -> (n u) (q h w)", u=HALVES)
    out_rows = out.rearrange("n c a b -> n (c a b)")


    with ExitStack() as ctx:
        keep = ctx.enter_context(tc.tile_pool(name="keep", bufs=1))
        big_pool = ctx.enter_context(tc.tile_pool(name="big", bufs=4))
        w_stage_pool = ctx.enter_context(tc.tile_pool(name="w_stage", bufs=1))
        sgn_pool = ctx.enter_context(tc.tile_pool(name="sgn", bufs=4))
        dz_pool = ctx.enter_context(tc.tile_pool(name="dz", bufs=3))
        work_pool = ctx.enter_context(tc.tile_pool(name="work", bufs=2))
        code_pool = ctx.enter_context(tc.tile_pool(name="code", bufs=3))
        turn_pool = ctx.enter_context(tc.psum_pool(name="turn", bufs=4))
        acc_pool = ctx.enter_context(tc.psum_pool(name="acc", bufs=4))

        def cuts(k):
            return ((0, C_LOAD // 2), (C_LOAD // 2, C_LOAD)) if k % 2 else ((0, C_LOAD),)

        def load_chunk(chunk):
            both = big_pool.tile([P, CHUNK_COLS + CHUNK_COLS // PAIR], F32, tag="big")
            z_t = both[:, 0:CHUNK_COLS]
            g_t = both[:, CHUNK_COLS:].bitcast(BF16)
            rows = slice(chunk * P, (chunk + 1) * P)
            for o0, o1 in pieces(chunk) if chunk == 0 or chunk % BLOCK_CHUNKS else [(0, O_HALF)]:
                cols = slice(o0 * PLACES, o1 * PLACES)
                nc.sync.dma_start(out=z_t[:, cols], in_=z_rows[rows, cols])
                nc.sync.dma_start(out=g_t[:, cols], in_=g_rows[rows, cols])
            return z_t, g_t

        def load_weights(k):
            raw = big_pool.tile([P, PACK, C_LOAD, PLACES * TAPS], BF16, tag="big")
            for c0, c1 in cuts(k):
                for u in range(HALVES):
                    nc.sync.dma_start(
                        out=raw[:, PAIR * u : PAIR * (u + 1), c0:c1, :],
                        in_=w_rows[:, u, :, k * C_LOAD + c0 : k * C_LOAD + c1, :],
                    )
            return raw

        loaded = []
        raws = []
        for part in range(PARTS):
            loaded.extend([load_chunk(part * BLOCK_CHUNKS + r) for r in range(BLOCK_CHUNKS)])
            raws.extend([load_weights(part * W_LOADS // PARTS + k) for k in range(W_LOADS // PARTS)])
        loaded.extend([load_chunk(chunk) for chunk in range(PARTS * BLOCK_CHUNKS, CHUNKS)])

        ident = keep.tile([P, P], F32)
        make_identity(nc, ident[:])
        ident_16 = keep.tile([P, P], BF16)
        make_identity(nc, ident_16[:])

        corner_cols = len(CORNER) * C
        w_codes = keep.tile([P, corner_cols + PARTS * PLACES * N_COLS], U32, align_bytes=64)
        w_scales = keep.tile([P, corner_cols + PARTS * PLACES * N_COLS], U8, align_bytes=64)

        def main_slots(plane):
            return plane[:, corner_cols:].rearrange(
                "p (f h w s c) -> p f h w s c", f=PARTS, h=SIDE, w=SIDE, s=SLOTS
            )

        for plane in (w_codes, w_scales):
            slots = main_slots(plane)
            nc.vector.memset(slots[:, :, :, 0, 2::SIDE, :].bitcast(I32), 0)
            nc.vector.memset(slots[:, :, :, 2, 0::SIDE, :].bitcast(I32), 0)
            nc.vector.memset(slots[:, :, 0, :, 2 * SIDE :, :].bitcast(I32), 0)
            nc.vector.memset(slots[:, :, 2, :, 0:SIDE, :].bitcast(I32), 0)

        def make_sign(chunk, piece):
            o0, o1 = piece
            sgn = sgn_pool.tile([P, (o1 - o0) * PLACES], BF16)
            nc.scalar.activation(
                out=sgn[:],
                in_=loaded[chunk][0][:, o0 * PLACES : o1 * PLACES],
                func=ACT.Sign,
                scale=SIGN_SCALE,
                bias=SIGN_BIAS,
            )
            return sgn

        def product(chunk, piece, h, sgn, dz):
            g_t = loaded[chunk][1]
            o0, o1 = piece
            cols = slice(o0 * PLACES, o1 * PLACES)
            nc.vector.scalar_tensor_tensor(
                out=dz[:, SIDE * h : SIDE * (h + 1), o0:o1].rearrange(
                    "q w p -> q p w"
                ),
                in0=sgn[:].rearrange("q (p h w) -> q h p w", h=SIDE, w=SIDE)[:, h, :, :],
                scalar=NEG_SLOPE,
                in1=g_t[:, cols].rearrange("q (p h w) -> q h p w", h=SIDE, w=SIDE)[:, h, :, :],
                op0=ALU.max,
                op1=ALU.mult,
            )

        def turn(dz, h, grouped, r):
            turned = turn_pool.tile([P, SIDE, P], F32)
            for i in range(SIDE):
                nc.tensor.transpose(turned[:, i, :], dz[:, SIDE * h + i, :].bitcast(F32), ident[:])
            nc.scalar.copy(out=grouped[:].bitcast(F32)[:, SIDE * h : SIDE * (h + 1), r, :], in_=turned[:])

        def quantise(grouped, h, dz_codes, dz_scales):
            for q0, q1 in ((SIDE * h, SIDE * h + 2), (SIDE * h + 2, SIDE * (h + 1))):
                nc.vector.quantize_mx(
                    out=dz_codes[:, q0:q1, :].rearrange("p s m -> p (s m)").bitcast(E5M2X4),
                    scales=dz_scales[:, q0:q1, :].rearrange("p s m -> p (s m)"),
                    in_=grouped[:, q0:q1, :, :].rearrange("p s r q -> p (s r q)"),
                )

        def one_pass(target, h, w, dz_codes, dz_scales, acc, start, stop):
            if target == LAST_PLACE:
                c0 = list(CORNER).index((h, w)) * C
            else:
                c0 = corner_cols + ((target * SIDE + h) * SIDE + w) * N_COLS
            nc.tensor.matmul_mx(
                out=acc[:],
                lhsT=dz_codes[:, SIDE * h + w, :].bitcast(E5M2X4),
                lhsT_scale=dz_scales[:, SIDE * h + w, :],
                rhs=w_codes[:, c0 : c0 + N_COLS].bitcast(E4M3X4),
                rhs_scale=w_scales[:, c0 : c0 + N_COLS],
                start=start,
                stop=stop,
            )

        def reaching(target):
            return CORNER if target == LAST_PLACE else [(h, w) for h in range(SIDE) for w in range(SIDE)]

        def bank_out(acc, target, padded):
            if target == LAST_PLACE:
                nc.scalar.copy(out=padded[:, :, SLOTS:PITCH], in_=acc[:].rearrange("n (s c) -> n c s", c=C))
            else:
                nc.scalar.copy(
                    out=padded[:, target * C_PART : (target + 1) * C_PART, 0:SLOTS],
                    in_=acc[:].rearrange("n (s c) -> n c s", c=C_PART),
                )

        def store(block, padded, c0=0, c1=C):
            result = work_pool.tile([P, (c1 - c0) * PLACES], F32)
            nc.vector.tensor_copy(
                out=result[:].rearrange("n (c s) -> n c s", s=PLACES),
                in_=padded[:, c0:c1, 0:PLACES],
            )
            nc.sync.dma_start(
                out=out_rows[block * P : (block + 1) * P, c0 * PLACES : c1 * PLACES], in_=result[:]
            )

        def prepare(block):
            grouped = work_pool.tile([P, PLACES, BLOCK_CHUNKS, PACK * CHUNK], BF16, align_bytes=64)
            dz_codes = code_pool.tile([P, PLACES, P], U32, align_bytes=64)
            dz_scales = code_pool.tile([P, PLACES, P], U8, align_bytes=64)
            for r in range(BLOCK_CHUNKS):
                chunk = block * BLOCK_CHUNKS + r
                dz = dz_pool.tile([P, PLACES, O_HALF], BF16)
                for piece in pieces(chunk):
                    sgn = make_sign(chunk, piece)
                    for h in range(SIDE):
                        product(chunk, piece, h, sgn, dz)
                for h in range(SIDE):
                    turn(dz, h, grouped, r)
                    if r == BLOCK_CHUNKS - 1:
                        quantise(grouped, h, dz_codes, dz_scales)
            return dz_codes, dz_scales

        def multiply(targets, dz_codes, dz_scales, padded):
            for target in targets:
                acc = acc_pool.tile([P, N_COLS], F32, tag="acc")
                places = reaching(target)
                for i, (h, w) in enumerate(places):
                    one_pass(target, h, w, dz_codes, dz_scales, acc, i == 0, i == len(places) - 1)
                bank_out(acc, target, padded)

        def prepare_by_rows(block):
            grouped = work_pool.tile([P, PLACES, BLOCK_CHUNKS, PACK * CHUNK], BF16, align_bytes=64)
            dz_codes = code_pool.tile([P, PLACES, P], U32, align_bytes=64)
            dz_scales = code_pool.tile([P, PLACES, P], U8, align_bytes=64)
            signs = {}
            turning = []
            for r in range(BLOCK_CHUNKS):
                dz = dz_pool.tile([P, PLACES, O_HALF], BF16)
                turning.append(dz)
                chunk = block * BLOCK_CHUNKS + r
                for piece in pieces(chunk):
                    signs[chunk, piece] = make_sign(chunk, piece)
            for h in range(SIDE):
                for r in range(BLOCK_CHUNKS):
                    chunk = block * BLOCK_CHUNKS + r
                    for piece in pieces(chunk):
                        product(chunk, piece, h, signs[chunk, piece], turning[r])
                for r in range(BLOCK_CHUNKS):
                    turn(turning[r], h, grouped, r)
                quantise(grouped, h, dz_codes, dz_scales)
            return dz_codes, dz_scales

        def multiply_by_rows(block, dz_codes, dz_scales, padded):
            gathering = {}
            for row in range(SIDE):
                for target in (LAST_PLACE, 0, 1):
                    places = reaching(target)
                    here = [(i, h, w) for i, (h, w) in enumerate(places) if h == row]
                    for i, h, w in here:
                        if i == 0:
                            acc = acc_pool.tile([P, N_COLS], F32, tag="acc")
                            gathering[target] = acc
                        one_pass(target, h, w, dz_codes, dz_scales, gathering[target], i == 0, i == len(places) - 1)
                    if row == SIDE - 1:
                        bank_out(gathering[target], target, padded)
                        if target != LAST_PLACE:
                            store(block, padded, target * C_PART, (target + 1) * C_PART)

        def quantise_slots(values, codes, scales):
            nc.vector.quantize_mx(
                out=codes.rearrange("p s c -> p (s c)").bitcast(E4M3X4),
                scales=scales.rearrange("p s c -> p (s c)"),
                in_=values.rearrange("p s x -> p (s x)"),
            )

        def weights(part):
            stages = {}
            for h in range(SIDE):
                for w in range(1, SIDE):
                    stages[h, w] = w_stage_pool.tile(
                        [P, len(near(h)), len(near(w)), C_PART, PACK], BF16, align_bytes=64, name="stage%d%d" % (h, w)
                    )
            left = w_stage_pool.tile([P, len(LEFT), PAIR, C_PART, PACK], BF16, align_bytes=64)
            loads = range(part * C_PART // C_LOAD, (part + 1) * C_PART // C_LOAD)
            for k, (c0, c1) in [(k, cut) for k in loads for cut in cuts(k)]:
                raw = raws[k][:, :, c0:c1, :]
                staged_c = slice(k * C_LOAD % C_PART + c0, k * C_LOAD % C_PART + c1)
                for i0 in range(0, len(LEFT), BANK_LEFT):
                    group = LEFT[i0 : i0 + BANK_LEFT]
                    words = acc_pool.tile([P, len(group), PAIR, c1 - c0, PACK], BF16, tag="acc", name="words")
                    for i, (h, a) in enumerate(group):
                        tap0 = SIDE * h * TAPS + SIDE * (a - h + 1) + 1
                        nc.tensor.matmul(
                            words[:, i, :, :, :],
                            lhsT=ident_16[:],
                            rhs=raw[:, :, :, tap0 : tap0 + PAIR].rearrange("p j c b -> p b c j"),
                            start=True,
                            stop=True,
                        )
                    nc.scalar.copy(
                        out=left[:, i0 : i0 + len(group), :, staged_c, :].rearrange(
                            "p i b c j -> p (i b) c j"
                        ),
                        in_=words[:].rearrange("p i b c j -> p (i b) c j"),
                    )
                for h in range(SIDE):
                    for w in range(1, SIDE):
                        rows, cols = near(h), near(w)
                        src = raw[:, :, :, (SIDE * h + w) * TAPS : (SIDE * h + w + 1) * TAPS].rearrange(
                            "p q c (i j) -> p q c i j", j=SIDE
                        )[:, :, :, rows[0] - h + 1 : rows[-1] - h + 2, cols[0] - w + 1 : cols[-1] - w + 2]
                        copy = nc.scalar.copy if w == 2 and h != 1 else nc.vector.tensor_copy
                        copy(
                            out=stages[h, w][:, :, :, staged_c, :].rearrange("p i b c q -> p i c b q"),
                            in_=src.rearrange("p q c i b -> p i c b q"),
                        )
            slots = [main_slots(plane)[:, part, :, :, :, :] for plane in (w_codes, w_scales)]
            corners = [
                plane[:, 0:corner_cols].rearrange("p (k f c) -> p k f c", f=PARTS, c=C_PART)[:, :, part, :]
                for plane in (w_codes, w_scales)
            ]
            for h in range(SIDE):
                for w in range(SIDE):
                    rows, cols = near(h), near(w)
                    if w == 0:
                        first = list(LEFT).index((h, rows[0]))
                        staged = left[:, first : first + len(rows), :, :, :]
                    else:
                        staged = stages[h, w][:]
                    staged = staged.rearrange("p i b c j -> p (i b) (c j)")
                    total = len(rows) * len(cols)
                    run = total if w == 1 else len(cols)
                    for i0 in range(0, total, run):
                        s0 = SIDE * (rows[0] + i0 // len(cols)) + cols[0]
                        left_over = min(run, SLOTS - s0)
                        i = i0
                        for n in (8, 4, 2, 1):
                            if left_over >= n:
                                s = s0 + i - i0
                                quantise_slots(
                                    staged[:, i : i + n, :],
                                    slots[0][:, h, w, s : s + n, :],
                                    slots[1][:, h, w, s : s + n, :],
                                )
                                i += n
                                left_over -= n
                    if (h, w) in CORNER:
                        k = list(CORNER).index((h, w))
                        quantise_slots(
                            staged[:, total - 1 : total, :], corners[0][:, k : k + 1, :], corners[1][:, k : k + 1, :]
                        )

        def pad():
            padded = work_pool.tile([P, C, PITCH], F32)
            return padded

        codes0 = prepare(0)
        weights(0)
        codes1 = prepare(1)
        pad0 = pad()
        multiply(TARGETS[:1], codes0[0], codes0[1], pad0)
        weights(1)
        pad1 = pad()
        multiply(TARGETS[:1], codes1[0], codes1[1], pad1)
        codes2 = prepare(2)
        multiply(TARGETS[1:], codes0[0], codes0[1], pad0)
        store(0, pad0)
        multiply(TARGETS[1:], codes1[0], codes1[1], pad1)
        store(1, pad1)
        codes3 = prepare_by_rows(3)
        pad2 = pad()
        multiply(TARGETS, codes2[0], codes2[1], pad2)
        store(2, pad2)
        pad3 = pad()
        multiply_by_rows(3, codes3[0], codes3[1], pad3)
